import numpy as np
import ml_dtypes


def mxq(x, axis, fmt="e4m3"):
    dtype, down = {"e4m3": (ml_dtypes.float8_e4m3fn, 7), "e5m2": (ml_dtypes.float8_e5m2, 14)}[fmt]
    v = np.moveaxis(np.asarray(x, np.float32).astype(ml_dtypes.bfloat16).astype(np.float64), axis, -1)
    blocks = v.reshape(v.shape[:-1] + (-1, 32))
    amax = np.abs(blocks).max(-1, keepdims=True)
    byte = np.maximum(np.where(amax > 0, np.frexp(amax)[1] - 1 + 127, 0) - down, 1)
    scale = np.exp2(byte - 127.0)
    codes = (blocks / scale).astype(np.float32).astype(dtype).astype(np.float64)
    return np.moveaxis((codes * scale).reshape(v.shape), -1, axis)


WIDE = False


def mx_kscale(k):
    if not WIDE:
        return np.ones(k)
    levels = np.array([10, -10, 5, -5, 0])
    a = np.random.permutation(np.resize(levels, k // 512 * 4)).reshape(k // 512, 4)
    idx = np.arange(k)
    return np.exp2(a[idx // 512, idx % 128 // 32])


BF16 = ml_dtypes.bfloat16


def bf(x):
    return np.asarray(x, np.float32).astype(BF16)


def f64(x):
    return np.asarray(x).astype(np.float64)


B, H, Wd, C_IN, KH, KW, OUT = 4, 32, 32, 456, 3, 3, 257
HCAT = (C_IN - 1) * KH * KW + 1
CURV = 1.0
SIG = 0.1004
HN = np.sqrt(1.0 / CURV + 2.0 * (HCAT - 1) * SIG ** 2)


def chan_scale():
    lv = np.unique(mx_kscale(HCAT))
    cyc = np.roll(np.concatenate([lv, lv[::-1]]), -(len(lv) // 2))
    return cyc[(np.arange(C_IN - 1) * len(cyc)) // (C_IN - 1)]


def setup_inputs():
    u = chan_scale()
    v = np.random.standard_normal((B, H, Wd, C_IN - 1)) * SIG
    t = np.sqrt(1.0 / CURV + np.sum(v * v, axis=-1, keepdims=True))
    s = np.concatenate([np.ones(1), np.tile(u, KH * KW)])
    return {"x": bf(np.concatenate([t, v * u], axis=-1)),
            "W": bf(np.random.standard_normal((OUT - 1, HCAT)) * (4.8 / (HN * np.sqrt(OUT - 1))) / s),
            "b": bf(np.random.standard_normal(OUT - 1) * (1.4 / np.sqrt(OUT - 1)))}


def reference(x, W, b):
    c = CURV
    x = f64(x)
    Bn, Hn, Wn, C = x.shape
    xp = np.pad(x, ((0, 0), (1, 1), (1, 1), (0, 0)), mode="edge")
    slabs = [xp[:, i:i + Hn, j:j + Wn, :] for i in range(KH) for j in range(KW)]
    patches = np.stack(slabs, axis=3)
    N = KH * KW
    t_cat = np.sqrt(np.sum(patches[..., 0] ** 2, axis=-1) - (N - 1) / c)
    sp = patches[..., 1:].reshape(Bn, Hn, Wn, N * (C - 1))
    h = np.concatenate([t_cat[..., None], sp], axis=-1)
    z = (mxq(h, 3, "e4m3") @ mxq(f64(W), 1, "e4m3").T) + f64(b)
    t_out = np.sqrt(1.0 / c + np.sum(z * z, axis=-1, keepdims=True))
    return np.concatenate([t_out, z], axis=-1)

@@ -1,0 +1,264 @@
+from contextlib import ExitStack
+
+import concourse.mybir as mybir
+from concourse.masks import make_identity
+
+F32 = mybir.dt.float32
+BF16 = mybir.dt.bfloat16
+U32 = mybir.dt.uint32
+U8 = mybir.dt.uint8
+FP8X4 = mybir.dt.float8_e4m3fn_x4
+ACT = mybir.ActivationFunctionType
+ALU = mybir.AluOpType
+
+P = 128
+NQ = 32
+CH = 456
+CPAD = 512
+OUT = 256
+TAPS = 9
+GQ = 4
+NG = NQ // GQ
+ROWS = 18
+COLW = ROWS * 8
+
+FLOPS = 2 * 4096 * 4096 * 256
+
+
+def tile_hypconvhyperboloid_kernel(tc, x, W, b, out):
+    nc = tc.nc
+    with ExitStack() as ctx:
+        const = ctx.enter_context(tc.tile_pool(name="const", bufs=1))
+        codes = ctx.enter_context(tc.tile_pool(name="codes", bufs=6))
+        outs = ctx.enter_context(tc.tile_pool(name="outs", bufs=3))
+        ps_tr = ctx.enter_context(tc.psum_pool(name="ps_tr", bufs=2))
+        ps_misc = ctx.enter_context(tc.psum_pool(name="ps_misc", bufs=2))
+        ps_z = ctx.enter_context(tc.psum_pool(name="ps_z", bufs=4))
+
+        x_rows = x.rearrange("b r q c -> (b r) q c")
+        out_rows = out.rearrange("b (h l) q c -> l (b h) (q c)", h=2, l=16)
+
+        xs = []
+        for g in range(NG):
+            xt = const.tile([P, GQ * CPAD], BF16, name="x%d" % g)
+            xs.append(xt)
+        wts = []
+        for ot in range(2):
+            wt = const.tile([P, TAPS * CPAD], BF16, name="wt%d" % ot)
+            wts.append(wt)
+
+        def load_x(g):
+            xv = xs[g][:].rearrange("p (k c) -> p k c", c=CPAD)
+            nc.vector.memset(xv[:, :, 448:CPAD], 0.0)
+            nc.sync.dma_start(out=xv[:, :, 0:CH], in_=x_rows[:, g * GQ : (g + 1) * GQ, :])
+
+        def load_w(ot):
+            wv = wts[ot][:].rearrange("p (n c) -> p n c", c=CPAD)
+            nc.vector.memset(wv[:, :, 448:CPAD], 0.0)
+            rows = W[ot * P : (ot + 1) * P, :]
+            nc.sync.dma_start(
+                out=wv[:, 0:8:2, 0:CH],
+                in_=rows[:, 0:3640].rearrange("o (m c) -> o m c", c=910)[:, :, 0:CH],
+            )
+            nc.sync.dma_start(
+                out=wv[:, 1:8:2, 0:CH],
+                in_=rows[:, 455:4095].rearrange("o (m c) -> o m c", c=910)[:, :, 0:CH],
+            )
+            nc.sync.dma_start(out=wv[:, 8, 0:CH], in_=rows[:, 3640:4096])
+            nc.vector.tensor_copy(out=wv[:, 4, 0:1], in_=wv[:, 0, 0:1])
+            nc.vector.memset(wv[:, 0:4, 0:1], 0.0)
+            nc.vector.memset(wv[:, 5:9, 0:1], 0.0)
+
+        load_x(0)
+        load_x(1)
+        load_x(2)
+        load_w(0)
+        load_w(1)
+        for g in range(3, NG):
+            load_x(g)
+
+        one1 = const.tile([P, 1], F32, name="one1")
+        nc.vector.memset(one1[:], 1.0)
+        neg8 = const.tile([P, 1], F32, name="neg8")
+        nc.vector.memset(neg8[:], -8.0)
+        warm = const.tile([P, 1], F32, name="warm")
+        nc.scalar.activation(out=warm[:], in_=one1[:], func=ACT.Sqrt)
+
+        ident = const.tile([P, P], F32, name="ident")
+        make_identity(nc, ident[:])
+        permf = const.tile([P, P], F32, name="permf")
+        nc.vector.tensor_copy(
+            out=permf[:].rearrange("k (l g) -> k l g", g=8),
+            in_=ident[:].rearrange("k (g l) -> k l g", l=16),
+        )
+        permb = const.tile([P, P], BF16, name="permb")
+        nc.vector.tensor_copy(out=permb[:], in_=permf[:])
+        band = const.tile([P, P], F32, name="band")
+        bv = band[:].rearrange("k (b r) -> k b r", r=32)
+        iv = ident[:].rearrange("k (b r) -> k b r", r=32)
+        nc.vector.tensor_copy(out=band[:], in_=ident[:])
+        nc.vector.tensor_tensor(out=bv[:, :, 1:32], in0=bv[:, :, 1:32], in1=iv[:, :, 0:31], op=ALU.add)
+        nc.vector.tensor_tensor(out=bv[:, :, 0:31], in0=bv[:, :, 0:31], in1=iv[:, :, 1:32], op=ALU.add)
+        nc.vector.tensor_tensor(out=bv[:, :, 0:32:31], in0=bv[:, :, 0:32:31], in1=iv[:, :, 0:32:31], op=ALU.add)
+
+        ones = const.tile([P, P], BF16, name="ones")
+        nc.vector.memset(ones[:], 1.0)
+        brow = const.tile([P, OUT], BF16, name="brow")
+        nc.vector.memset(brow[:], 0.0)
+        nc.scalar.dma_start(out=brow[0:1, :], in_=b.unsqueeze(0))
+        bbc = const.tile([P, 2 * OUT], F32, name="bbc")
+        bps = ps_misc.tile([P, 512], F32, tag="misc", name="bps")
+        nc.tensor.matmul(out=bps[:, 0:OUT], lhsT=ones[:], rhs=brow[:], start=True, stop=True)
+        nc.scalar.copy(out=bbc[:, 0:OUT], in_=bps[:, 0:OUT])
+        nc.scalar.copy(out=bbc[:, OUT : 2 * OUT], in_=bps[:, 0:OUT])
+
+        sq = const.tile([P, NQ + 2], F32, name="sq")
+        tcat = const.tile([P, NQ], BF16, name="tcat")
+        ts = []
+        for g in range(NG):
+            tt = const.tile([P, GQ * COLW * 4], BF16, name="t%d" % g, align_bytes=64)
+            ts.append(tt)
+
+        def squares(g):
+            xv = xs[g][:].rearrange("p (k c) -> p k c", c=CPAD)
+            nc.scalar.activation(out=sq[:, 1 + g * GQ : 1 + (g + 1) * GQ], in_=xv[:, :, 0], func=ACT.Square)
+
+        def prep(g):
+            xf = xs[g][:].bitcast(F32).rearrange("p (k w u) -> p k w u", w=P, u=2)
+            t32 = ts[g][:].bitcast(F32)
+            t32v = t32.rearrange("p (k w) -> p k w", w=COLW * 2)
+            for h in range(GQ // 2):
+                tr = ps_tr.tile([P, 512], F32, tag="tr", name="tr")
+                for k in range(2):
+                    for u in range(2):
+                        s = 2 * k + u
+                        nc.tensor.transpose(tr[:, s * P : (s + 1) * P], xf[:, 2 * h + k, :, u], permf[:])
+                nc.scalar.copy(
+                    out=t32v[:, 2 * h : 2 * h + 2, 16:272].rearrange("p k (w u) -> p k w u", u=2),
+                    in_=tr[:].rearrange("p (k u w) -> p k w u", k=2, u=2),
+                )
+            t6 = t32.rearrange("p (k r b h u) -> p k r b h u", r=ROWS, b=4, h=2, u=2)
+            for dst, hs in ((0, 0), (ROWS - 1, 1)):
+                nc.scalar.copy(
+                    out=t6[:, :, dst, :, :, :],
+                    in_=t6[:, :, 1:17:15, :, hs, :].rearrange("p k r b u -> p k b r u"),
+                )
+            if g == 0:
+                squares(0)
+                nc.scalar.copy(out=sq[:, 0:1], in_=sq[:, 1:2])
+            if g + 1 < NG:
+                squares(g + 1)
+            else:
+                nc.scalar.copy(out=sq[:, NQ + 1 : NQ + 2], in_=sq[:, NQ : NQ + 1])
+            sps = ps_misc.tile([P, 512], F32, tag="misc", name="sps")
+            for j in range(3):
+                nc.tensor.matmul(
+                    out=sps[:, 0:GQ],
+                    lhsT=band[:],
+                    rhs=sq[:, g * GQ + j : g * GQ + j + GQ],
+                    start=(j == 0),
+                    stop=(j == 2),
+                )
+            nc.scalar.activation(
+                out=tcat[:, g * GQ : (g + 1) * GQ], in_=sps[:, 0:GQ], func=ACT.Sqrt, bias=neg8[:], scale=1.0
+            )
+            rows = ps_misc.tile([P, 512], F32, tag="misc", name="rows")
+            for k in range(GQ):
+                nc.tensor.matmul(
+                    out=rows[:, k * P : (k + 1) * P],
+                    lhsT=tcat[:, g * GQ + k : g * GQ + k + 1].to_broadcast([P, P]),
+                    rhs=permb[:],
+                    start=True,
+                    stop=True,
+                )
+            tv = ts[g][:].rearrange("p (k w t) -> p k w t", w=COLW, t=4)
+            nc.scalar.copy(out=tv[0:1, :, 8:136, 0], in_=rows[0:1, :].rearrange("p (k w) -> p k w", k=GQ))
+
+        wg = const.tile([P, TAPS * OUT * 4], BF16, name="wg", align_bytes=64)
+        wc = const.tile([P, TAPS * OUT], U32, name="wc", align_bytes=64)
+        ws = const.tile([P, TAPS * OUT], U8, name="ws", align_bytes=64)
+
+        def weights():
+            wg32 = wg[:].bitcast(F32)
+            wf = [wts[ot][:].bitcast(F32).rearrange("p (n w u) -> p n w u", w=P, u=2) for ot in range(2)]
+            for n in range(TAPS):
+                tr = ps_tr.tile([P, 512], F32, tag="tr", name="trw")
+                for ot in range(2):
+                    for u in range(2):
+                        s = 2 * ot + u
+                        nc.tensor.transpose(tr[:, s * P : (s + 1) * P], wf[ot][:, n, :, u], ident[:])
+                dst = wg32[:, n * 512 : (n + 1) * 512].rearrange("p (t o u) -> p t o u", t=2, u=2)
+                src = tr[:].rearrange("p (t u o) -> p t o u", t=2, u=2)
+                if n % 2 == 0:
+                    nc.vector.tensor_copy(out=dst, in_=src)
+                else:
+                    nc.scalar.copy(out=dst, in_=src)
+            for n in range(TAPS):
+                nc.vector.quantize_mx(
+                    out=wc[:, n * OUT : (n + 1) * OUT].bitcast(FP8X4),
+                    scales=ws[:, n * OUT : (n + 1) * OUT],
+                    in_=wg[:, n * OUT * 4 : (n + 1) * OUT * 4],
+                )
+
+        state = {}
+
+        def pixel(q):
+            cod = codes.tile([P, TAPS * P], U32, tag="cod", name="cod", align_bytes=64)
+            scl = codes.tile([P, TAPS * P], U8, tag="scl", name="scl", align_bytes=64)
+            for n in range(TAPS):
+                i, j = divmod(n, 3)
+                g, k = divmod(min(max(q + j - 1, 0), NQ - 1), GQ)
+                base = (k * COLW + i * 8) * 4
+                nc.vector.quantize_mx(
+                    out=cod[:, n * P : (n + 1) * P].bitcast(FP8X4),
+                    scales=scl[:, n * P : (n + 1) * P],
+                    in_=ts[g][:, base : base + 512],
+                )
+            half = q % 2
+            if half == 0:
+                state["z"] = ps_z.tile([P, 512], F32, tag="z", name="z")
+            z = state["z"]
+            for n in range(TAPS):
+                nc.tensor.matmul_mx(
+                    out=z[:, half * OUT : (half + 1) * OUT],
+                    lhsT=cod[:, n * P : (n + 1) * P].bitcast(FP8X4),
+                    lhsT_scale=scl[:, n * P : (n + 1) * P],
+                    rhs=wc[:, n * OUT : (n + 1) * OUT].bitcast(FP8X4),
+                    rhs_scale=ws[:, n * OUT : (n + 1) * OUT],
+                    start=(n == 0),
+                    stop=(n == TAPS - 1),
+                )
+            if half == 0:
+                return
+            s = q % 8
+            if s == 1:
+                state["o"] = outs.tile([P, 8, OUT + 1], F32, tag="o", name="o")
+                state["ss"] = outs.tile([P, 8], F32, tag="ss", name="ss")
+            o = state["o"]
+            ss = state["ss"]
+            nc.vector.tensor_tensor(
+                out=o[:, s - 1 : s + 1, 1 : OUT + 1],
+                in0=z[:].rearrange("p (k n) -> p k n", k=2),
+                in1=bbc[:].rearrange("p (k n) -> p k n", k=2),
+                op=ALU.add,
+            )
+            for k in (s - 1, s):
+                junk = outs.tile([P, OUT], BF16, tag="junk", name="junk")
+                nc.scalar.activation(
+                    out=junk[:], in_=o[:, k, 1 : OUT + 1], func=ACT.Square, accum_out=ss[:, k : k + 1]
+                )
+            if s == 7:
+                nc.scalar.activation(out=o[:, :, 0], in_=ss[:], func=ACT.Sqrt, bias=one1[:], scale=1.0)
+                nc.sync.dma_start(
+                    out=out_rows[:, :, (q - 7) * (OUT + 1) : (q + 1) * (OUT + 1)],
+                    in_=o[:].rearrange("p q c -> p (q c)"),
+                )
+
+        prep(0)
+        prep(1)
+        weights()
+        for g in range(NG):
+            if g + 2 < NG:
+                prep(g + 2)
+            for q in range(g * GQ, (g + 1) * GQ):
+                pixel(q)

@@ -17,10 +17,12 @@ CH = 456
 CPAD = 512
 OUT = 256
 TAPS = 9
-GQ = 4
-NG = NQ // GQ
 ROWS = 18
 COLW = ROWS * 8
+CHUNKS = (0, 5, 9, 17, 25, 32)
+BATCHES = ((0, 4), (4, 8), (8, 16), (16, 32))
+SLOT = (0, 4, 1, 5, 2, 6, 3, 7, 8)
+LAG = 2
 
 FLOPS = 2 * 4096 * 4096 * 256
 
@@ -28,54 +30,52 @@ FLOPS = 2 * 4096 * 4096 * 256
 def tile_hypconvhyperboloid_kernel(tc, x, W, b, out):
     nc = tc.nc
     with ExitStack() as ctx:
+        ctx.enter_context(tc.manual_schedule())
         const = ctx.enter_context(tc.tile_pool(name="const", bufs=1))
-        codes = ctx.enter_context(tc.tile_pool(name="codes", bufs=6))
-        outs = ctx.enter_context(tc.tile_pool(name="outs", bufs=3))
-        ps_tr = ctx.enter_context(tc.psum_pool(name="ps_tr", bufs=2))
+        codes = ctx.enter_context(tc.tile_pool(name="codes", bufs=8))
+        outs = ctx.enter_context(tc.tile_pool(name="outs", bufs=2))
+        ps_tr = ctx.enter_context(tc.psum_pool(name="ps_tr", bufs=3))
         ps_misc = ctx.enter_context(tc.psum_pool(name="ps_misc", bufs=2))
-        ps_z = ctx.enter_context(tc.psum_pool(name="ps_z", bufs=4))
+        ps_z = ctx.enter_context(tc.psum_pool(name="ps_z", bufs=3))
 
         x_rows = x.rearrange("b r q c -> (b r) q c")
         out_rows = out.rearrange("b (h l) q c -> l (b h) (q c)", h=2, l=16)
 
         xs = []
-        for g in range(NG):
-            xt = const.tile([P, GQ * CPAD], BF16, name="x%d" % g)
+        for c in range(5):
+            xt = const.tile([P, (CHUNKS[c + 1] - CHUNKS[c]) * CPAD], BF16, name="x%d" % c)
             xs.append(xt)
         wts = []
         for ot in range(2):
             wt = const.tile([P, TAPS * CPAD], BF16, name="wt%d" % ot)
             wts.append(wt)
+        wvs = [wts[ot][:].rearrange("p (n c) -> p n c", c=CPAD) for ot in range(2)]
 
-        def load_x(g):
-            xv = xs[g][:].rearrange("p (k c) -> p k c", c=CPAD)
+        def load_x(c):
+            xv = xs[c][:].rearrange("p (k c) -> p k c", c=CPAD)
             nc.vector.memset(xv[:, :, 448:CPAD], 0.0)
-            nc.sync.dma_start(out=xv[:, :, 0:CH], in_=x_rows[:, g * GQ : (g + 1) * GQ, :])
+            nc.sync.dma_start(out=xv[:, :, 0:CH], in_=x_rows[:, CHUNKS[c] : CHUNKS[c + 1], :])
 
-        def load_w(ot):
-            wv = wts[ot][:].rearrange("p (n c) -> p n c", c=CPAD)
-            nc.vector.memset(wv[:, :, 448:CPAD], 0.0)
-            rows = W[ot * P : (ot + 1) * P, :]
-            nc.sync.dma_start(
-                out=wv[:, 0:8:2, 0:CH],
-                in_=rows[:, 0:3640].rearrange("o (m c) -> o m c", c=910)[:, :, 0:CH],
-            )
-            nc.sync.dma_start(
-                out=wv[:, 1:8:2, 0:CH],
-                in_=rows[:, 455:4095].rearrange("o (m c) -> o m c", c=910)[:, :, 0:CH],
-            )
-            nc.sync.dma_start(out=wv[:, 8, 0:CH], in_=rows[:, 3640:4096])
-            nc.vector.tensor_copy(out=wv[:, 4, 0:1], in_=wv[:, 0, 0:1])
-            nc.vector.memset(wv[:, 0:4, 0:1], 0.0)
-            nc.vector.memset(wv[:, 5:9, 0:1], 0.0)
-
+        brow = const.tile([P, OUT], BF16, name="brow")
+        nc.vector.memset(brow[:], 0.0)
+        nc.scalar.dma_start(out=brow[0:1, :], in_=b.unsqueeze(0))
         load_x(0)
-        load_x(1)
-        load_x(2)
-        load_w(0)
-        load_w(1)
-        for g in range(3, NG):
-            load_x(g)
+        for ot in range(2):
+            nc.vector.memset(wvs[ot][:, :, 448:CPAD], 0.0)
+        for ot in range(2):
+            nc.sync.dma_start(
+                out=wvs[ot][:, 0:8:2, 0:CH],
+                in_=W[ot * P : (ot + 1) * P, 0:3640].rearrange("o (m c) -> o m c", c=910)[:, :, 0:CH],
+            )
+        for ot in range(2):
+            nc.sync.dma_start(
+                out=wvs[ot][:, 1:8:2, 0:CH],
+                in_=W[ot * P : (ot + 1) * P, 455:4095].rearrange("o (m c) -> o m c", c=910)[:, :, 0:CH],
+            )
+        for ot in range(2):
+            nc.sync.dma_start(out=wvs[ot][:, 8, 0:CH], in_=W[ot * P : (ot + 1) * P, 3640:4096])
+        for c in range(1, 5):
+            load_x(c)
 
         one1 = const.tile([P, 1], F32, name="one1")
         nc.vector.memset(one1[:], 1.0)
@@ -91,8 +91,6 @@ def tile_hypconvhyperboloid_kernel(tc, x, W, b, out):
             out=permf[:].rearrange("k (l g) -> k l g", g=8),
             in_=ident[:].rearrange("k (g l) -> k l g", l=16),
         )
-        permb = const.tile([P, P], BF16, name="permb")
-        nc.vector.tensor_copy(out=permb[:], in_=permf[:])
         band = const.tile([P, P], F32, name="band")
         bv = band[:].rearrange("k (b r) -> k b r", r=32)
         iv = ident[:].rearrange("k (b r) -> k b r", r=32)
@@ -100,165 +98,249 @@ def tile_hypconvhyperboloid_kernel(tc, x, W, b, out):
         nc.vector.tensor_tensor(out=bv[:, :, 1:32], in0=bv[:, :, 1:32], in1=iv[:, :, 0:31], op=ALU.add)
         nc.vector.tensor_tensor(out=bv[:, :, 0:31], in0=bv[:, :, 0:31], in1=iv[:, :, 1:32], op=ALU.add)
         nc.vector.tensor_tensor(out=bv[:, :, 0:32:31], in0=bv[:, :, 0:32:31], in1=iv[:, :, 0:32:31], op=ALU.add)
-
+        permb = const.tile([P, P], BF16, name="permb")
+        nc.vector.tensor_copy(out=permb[:], in_=permf[:])
         ones = const.tile([P, P], BF16, name="ones")
         nc.vector.memset(ones[:], 1.0)
-        brow = const.tile([P, OUT], BF16, name="brow")
-        nc.vector.memset(brow[:], 0.0)
-        nc.scalar.dma_start(out=brow[0:1, :], in_=b.unsqueeze(0))
-        bbc = const.tile([P, 2 * OUT], F32, name="bbc")
-        bps = ps_misc.tile([P, 512], F32, tag="misc", name="bps")
-        nc.tensor.matmul(out=bps[:, 0:OUT], lhsT=ones[:], rhs=brow[:], start=True, stop=True)
-        nc.scalar.copy(out=bbc[:, 0:OUT], in_=bps[:, 0:OUT])
-        nc.scalar.copy(out=bbc[:, OUT : 2 * OUT], in_=bps[:, 0:OUT])
 
+        for ot in range(2):
+            nc.gpsimd.tensor_copy(out=wvs[ot][:, 4, 0:1], in_=wvs[ot][:, 0, 0:1])
+            nc.gpsimd.memset(wvs[ot][:, 0:4:2, 0:1], 0.0)
+            nc.gpsimd.memset(wvs[ot][:, 6:7, 0:1], 0.0)
+        for ot in range(2):
+            nc.gpsimd.memset(wvs[ot][:, 1:8:2, 0:1], 0.0)
+        for ot in range(2):
+            nc.gpsimd.memset(wvs[ot][:, 8:9, 0:1], 0.0)
+
+        bbc = const.tile([P, 2 * OUT], F32, name="bbc")
         sq = const.tile([P, NQ + 2], F32, name="sq")
         tcat = const.tile([P, NQ], BF16, name="tcat")
         ts = []
-        for g in range(NG):
-            tt = const.tile([P, GQ * COLW * 4], BF16, name="t%d" % g, align_bytes=64)
+        for pr in range(NQ // 2):
+            tt = const.tile([P, 2 * COLW * 4], BF16, name="t%d" % pr, align_bytes=64)
             ts.append(tt)
+        wg = const.tile([P, TAPS * OUT * 4], BF16, name="wg", align_bytes=64)
+        wc = const.tile([P, TAPS * OUT], U32, name="wc", align_bytes=64)
+        ws = const.tile([P, TAPS * OUT], U8, name="ws", align_bytes=64)
+        state = {}
 
-        def squares(g):
-            xv = xs[g][:].rearrange("p (k c) -> p k c", c=CPAD)
-            nc.scalar.activation(out=sq[:, 1 + g * GQ : 1 + (g + 1) * GQ], in_=xv[:, :, 0], func=ACT.Square)
+        def x_words(col, u):
+            c = max(i for i in range(5) if CHUNKS[i] <= col)
+            xf = xs[c][:].bitcast(F32).rearrange("p (k w u) -> p k w u", w=P, u=2)
+            return xf[:, col - CHUNKS[c], :, u]
 
-        def prep(g):
-            xf = xs[g][:].bitcast(F32).rearrange("p (k w u) -> p k w u", w=P, u=2)
-            t32 = ts[g][:].bitcast(F32)
-            t32v = t32.rearrange("p (k w) -> p k w", w=COLW * 2)
-            for h in range(GQ // 2):
-                tr = ps_tr.tile([P, 512], F32, tag="tr", name="tr")
-                for k in range(2):
-                    for u in range(2):
-                        s = 2 * k + u
-                        nc.tensor.transpose(tr[:, s * P : (s + 1) * P], xf[:, 2 * h + k, :, u], permf[:])
-                nc.scalar.copy(
-                    out=t32v[:, 2 * h : 2 * h + 2, 16:272].rearrange("p k (w u) -> p k w u", u=2),
-                    in_=tr[:].rearrange("p (k u w) -> p k w u", k=2, u=2),
-                )
+        def squares(c):
+            xv = xs[c][:].rearrange("p (k c) -> p k c", c=CPAD)
+            nc.scalar.activation(out=sq[:, 1 + CHUNKS[c] : 1 + CHUNKS[c + 1]], in_=xv[:, :, 0], func=ACT.Square)
+            if c == 0:
+                nc.scalar.copy(out=sq[:, 0:1], in_=sq[:, 1:2])
+            if c == 4:
+                nc.scalar.copy(out=sq[:, NQ + 1 : NQ + 2], in_=sq[:, NQ : NQ + 1])
+
+        def transposes(pr):
+            tr = ps_tr.tile([P, 512], F32, tag="tr", name="tr")
+            for k in range(2):
+                for u in range(2):
+                    s = 2 * k + u
+                    nc.tensor.transpose(tr[:, s * P : (s + 1) * P], x_words(2 * pr + k, u), permf[:])
+            state["tr%d" % pr] = tr
+
+        def copy_on(eng, dst, src):
+            if eng == "v":
+                nc.vector.tensor_copy(out=dst, in_=src)
+            else:
+                nc.scalar.copy(out=dst, in_=src)
+
+        def copy_out(pr, eng):
+            t32 = ts[pr][:].bitcast(F32)
+            copy_on(
+                eng,
+                t32.rearrange("p (k w) -> p k w", w=COLW * 2)[:, :, 16:272].rearrange("p k (w u) -> p k w u", u=2),
+                state["tr%d" % pr][:].rearrange("p (k u w) -> p k w u", k=2, u=2),
+            )
             t6 = t32.rearrange("p (k r b h u) -> p k r b h u", r=ROWS, b=4, h=2, u=2)
             for dst, hs in ((0, 0), (ROWS - 1, 1)):
-                nc.scalar.copy(
-                    out=t6[:, :, dst, :, :, :],
-                    in_=t6[:, :, 1:17:15, :, hs, :].rearrange("p k r b u -> p k b r u"),
-                )
-            if g == 0:
-                squares(0)
-                nc.scalar.copy(out=sq[:, 0:1], in_=sq[:, 1:2])
-            if g + 1 < NG:
-                squares(g + 1)
-            else:
-                nc.scalar.copy(out=sq[:, NQ + 1 : NQ + 2], in_=sq[:, NQ : NQ + 1])
+                copy_on(eng, t6[:, :, dst, :, :, :], t6[:, :, 1:17:15, :, hs, :].rearrange("p k r b u -> p k b r u"))
+
+        def sums(bt):
+            lo, hi = BATCHES[bt]
             sps = ps_misc.tile([P, 512], F32, tag="misc", name="sps")
             for j in range(3):
                 nc.tensor.matmul(
-                    out=sps[:, 0:GQ],
-                    lhsT=band[:],
-                    rhs=sq[:, g * GQ + j : g * GQ + j + GQ],
-                    start=(j == 0),
-                    stop=(j == 2),
+                    out=sps[:, 0 : hi - lo], lhsT=band[:], rhs=sq[:, lo + j : hi + j], start=(j == 0), stop=(j == 2)
                 )
+            state["sps%d" % bt] = sps
+
+        def roots(bt):
+            lo, hi = BATCHES[bt]
             nc.scalar.activation(
-                out=tcat[:, g * GQ : (g + 1) * GQ], in_=sps[:, 0:GQ], func=ACT.Sqrt, bias=neg8[:], scale=1.0
+                out=tcat[:, lo:hi], in_=state["sps%d" % bt][:, 0 : hi - lo], func=ACT.Sqrt, bias=neg8[:], scale=1.0
             )
-            rows = ps_misc.tile([P, 512], F32, tag="misc", name="rows")
-            for k in range(GQ):
+
+        def rows(g):
+            rw = ps_misc.tile([P, 512], F32, tag="misc", name="rw")
+            for k in range(4):
                 nc.tensor.matmul(
-                    out=rows[:, k * P : (k + 1) * P],
-                    lhsT=tcat[:, g * GQ + k : g * GQ + k + 1].to_broadcast([P, P]),
+                    out=rw[:, k * P : (k + 1) * P],
+                    lhsT=tcat[:, 4 * g + k : 4 * g + k + 1].to_broadcast([P, P]),
                     rhs=permb[:],
                     start=True,
                     stop=True,
                 )
-            tv = ts[g][:].rearrange("p (k w t) -> p k w t", w=COLW, t=4)
-            nc.scalar.copy(out=tv[0:1, :, 8:136, 0], in_=rows[0:1, :].rearrange("p (k w) -> p k w", k=GQ))
+            state["rw%d" % g] = rw
 
-        wg = const.tile([P, TAPS * OUT * 4], BF16, name="wg", align_bytes=64)
-        wc = const.tile([P, TAPS * OUT], U32, name="wc", align_bytes=64)
-        ws = const.tile([P, TAPS * OUT], U8, name="ws", align_bytes=64)
+        def row_write(pr, eng):
+            tv = ts[pr][:].rearrange("p (k w t) -> p k w t", w=COLW, t=4)
+            half = pr % 2
+            copy_on(
+                eng,
+                tv[0:1, :, 8:136, 0],
+                state["rw%d" % (pr // 2)][0:1, half * 256 : (half + 1) * 256].rearrange("p (k w) -> p k w", k=2),
+            )
 
-        def weights():
+        def weight_tap(n):
             wg32 = wg[:].bitcast(F32)
-            wf = [wts[ot][:].bitcast(F32).rearrange("p (n w u) -> p n w u", w=P, u=2) for ot in range(2)]
-            for n in range(TAPS):
-                tr = ps_tr.tile([P, 512], F32, tag="tr", name="trw")
-                for ot in range(2):
-                    for u in range(2):
-                        s = 2 * ot + u
-                        nc.tensor.transpose(tr[:, s * P : (s + 1) * P], wf[ot][:, n, :, u], ident[:])
-                dst = wg32[:, n * 512 : (n + 1) * 512].rearrange("p (t o u) -> p t o u", t=2, u=2)
-                src = tr[:].rearrange("p (t u o) -> p t o u", t=2, u=2)
-                if n % 2 == 0:
-                    nc.vector.tensor_copy(out=dst, in_=src)
-                else:
-                    nc.scalar.copy(out=dst, in_=src)
-            for n in range(TAPS):
-                nc.vector.quantize_mx(
-                    out=wc[:, n * OUT : (n + 1) * OUT].bitcast(FP8X4),
-                    scales=ws[:, n * OUT : (n + 1) * OUT],
-                    in_=wg[:, n * OUT * 4 : (n + 1) * OUT * 4],
-                )
+            tr = ps_tr.tile([P, 512], F32, tag="tr", name="trw")
+            for ot in range(2):
+                wf = wts[ot][:].bitcast(F32).rearrange("p (n w u) -> p n w u", w=P, u=2)
+                for u in range(2):
+                    s = 2 * ot + u
+                    nc.tensor.transpose(tr[:, s * P : (s + 1) * P], wf[:, n, :, u], ident[:])
+            nc.scalar.copy(
+                out=wg32[:, SLOT[n] * 512 : (SLOT[n] + 1) * 512].rearrange("p (t o u) -> p t o u", t=2, u=2),
+                in_=tr[:].rearrange("p (t u o) -> p t o u", t=2, u=2),
+            )
 
-        state = {}
+        def weight_quant(s0, s1):
+            nc.vector.quantize_mx(
+                out=wc[:, s0 * OUT : s1 * OUT].bitcast(FP8X4),
+                scales=ws[:, s0 * OUT : s1 * OUT],
+                in_=wg[:, s0 * OUT * 4 : s1 * OUT * 4],
+            )
 
-        def pixel(q):
+        def shared(q, n):
+            return (q == 1 and n % 3 == 0) or (q == NQ - 1 and n % 3 == 2)
+
+        def quant(q):
             cod = codes.tile([P, TAPS * P], U32, tag="cod", name="cod", align_bytes=64)
             scl = codes.tile([P, TAPS * P], U8, tag="scl", name="scl", align_bytes=64)
+            state["cod%d" % q] = cod
+            state["scl%d" % q] = scl
             for n in range(TAPS):
+                if shared(q, n):
+                    continue
                 i, j = divmod(n, 3)
-                g, k = divmod(min(max(q + j - 1, 0), NQ - 1), GQ)
+                pr, k = divmod(min(max(q + j - 1, 0), NQ - 1), 2)
                 base = (k * COLW + i * 8) * 4
                 nc.vector.quantize_mx(
                     out=cod[:, n * P : (n + 1) * P].bitcast(FP8X4),
                     scales=scl[:, n * P : (n + 1) * P],
-                    in_=ts[g][:, base : base + 512],
+                    in_=ts[pr][:, base : base + 512],
                 )
+
+        def passes(q):
             half = q % 2
             if half == 0:
-                state["z"] = ps_z.tile([P, 512], F32, tag="z", name="z")
-            z = state["z"]
+                state["z%d" % (q // 2)] = ps_z.tile([P, 512], F32, tag="z", name="z")
+            z = state["z%d" % (q // 2)]
             for n in range(TAPS):
+                src = q - 1 if shared(q, n) else q
+                s = SLOT[n]
                 nc.tensor.matmul_mx(
                     out=z[:, half * OUT : (half + 1) * OUT],
-                    lhsT=cod[:, n * P : (n + 1) * P].bitcast(FP8X4),
-                    lhsT_scale=scl[:, n * P : (n + 1) * P],
-                    rhs=wc[:, n * OUT : (n + 1) * OUT].bitcast(FP8X4),
-                    rhs_scale=ws[:, n * OUT : (n + 1) * OUT],
+                    lhsT=state["cod%d" % src][:, n * P : (n + 1) * P].bitcast(FP8X4),
+                    lhsT_scale=state["scl%d" % src][:, n * P : (n + 1) * P],
+                    rhs=wc[:, s * OUT : (s + 1) * OUT].bitcast(FP8X4),
+                    rhs_scale=ws[:, s * OUT : (s + 1) * OUT],
                     start=(n == 0),
                     stop=(n == TAPS - 1),
                 )
-            if half == 0:
-                return
-            s = q % 8
-            if s == 1:
+
+        def finish(pp):
+            s = (2 * pp) % 8
+            if s == 0:
                 state["o"] = outs.tile([P, 8, OUT + 1], F32, tag="o", name="o")
                 state["ss"] = outs.tile([P, 8], F32, tag="ss", name="ss")
             o = state["o"]
             ss = state["ss"]
             nc.vector.tensor_tensor(
-                out=o[:, s - 1 : s + 1, 1 : OUT + 1],
-                in0=z[:].rearrange("p (k n) -> p k n", k=2),
+                out=o[:, s : s + 2, 1 : OUT + 1],
+                in0=state["z%d" % pp][:].rearrange("p (k n) -> p k n", k=2),
                 in1=bbc[:].rearrange("p (k n) -> p k n", k=2),
                 op=ALU.add,
             )
-            for k in (s - 1, s):
+            for k in (s, s + 1):
                 junk = outs.tile([P, OUT], BF16, tag="junk", name="junk")
                 nc.scalar.activation(
                     out=junk[:], in_=o[:, k, 1 : OUT + 1], func=ACT.Square, accum_out=ss[:, k : k + 1]
                 )
-            if s == 7:
+            if s == 6:
+                q0 = 2 * pp - 6
                 nc.scalar.activation(out=o[:, :, 0], in_=ss[:], func=ACT.Sqrt, bias=one1[:], scale=1.0)
                 nc.sync.dma_start(
-                    out=out_rows[:, :, (q - 7) * (OUT + 1) : (q + 1) * (OUT + 1)],
+                    out=out_rows[:, :, q0 * (OUT + 1) : (q0 + 8) * (OUT + 1)],
                     in_=o[:].rearrange("p q c -> p (q c)"),
                 )
 
-        prep(0)
-        prep(1)
-        weights()
-        for g in range(NG):
-            if g + 2 < NG:
-                prep(g + 2)
-            for q in range(g * GQ, (g + 1) * GQ):
-                pixel(q)
+        squares(0)
+        transposes(0)
+        sums(0)
+        copy_out(0, "a")
+        roots(0)
+        transposes(1)
+        rows(0)
+        row_write(0, "a")
+        copy_out(1, "v")
+        row_write(1, "v")
+        quant(0)
+        quant(1)
+        quant(2)
+        for n in (0, 2, 4, 6):
+            weight_tap(n)
+        weight_quant(0, 4)
+        for n in (1, 3, 5, 7, 8):
+            weight_tap(n)
+        weight_quant(4, 8)
+        weight_quant(8, 9)
+        bps = ps_misc.tile([P, 512], F32, tag="misc", name="bps")
+        nc.tensor.matmul(out=bps[:, 0:OUT], lhsT=ones[:], rhs=brow[:], start=True, stop=True)
+        nc.scalar.copy(out=bbc[:, 0:OUT], in_=bps[:, 0:OUT])
+        nc.scalar.copy(out=bbc[:, OUT : 2 * OUT], in_=bps[:, 0:OUT])
+        squares(1)
+        squares(2)
+        transposes(2)
+        sums(1)
+        transposes(3)
+        copy_out(2, "a")
+        roots(1)
+        rows(1)
+        sums(2)
+        row_write(2, "a")
+        copy_out(3, "a")
+        row_write(3, "a")
+        roots(2)
+
+        for blk in range(8):
+            g = blk + 2
+            if g < 8:
+                if blk == 1:
+                    sums(3)
+                    roots(3)
+                transposes(2 * g)
+                transposes(2 * g + 1)
+                rows(g)
+                for pr in (2 * g, 2 * g + 1):
+                    copy_out(pr, "a")
+                for pr in (2 * g, 2 * g + 1):
+                    row_write(pr, "a")
+                if blk == 0:
+                    squares(3)
+                    squares(4)
+            for q in range(4 * blk, 4 * blk + 4):
+                if q > 2:
+                    quant(q)
+                passes(q)
+                if q % 2 == 1 and q // 2 - LAG >= 0:
+                    finish(q // 2 - LAG)
+        for pp in range(NQ // 2 - LAG, NQ // 2):
+            finish(pp)

@@ -22,6 +22,7 @@ COLW = ROWS * 8
 CHUNKS = (0, 5, 9, 17, 25, 32)
 BATCHES = ((0, 4), (4, 8), (8, 16), (16, 32))
 SLOT = (0, 4, 1, 5, 2, 6, 3, 7, 8)
+SHIFT = 48
 LAG = 2
 
 FLOPS = 2 * 4096 * 4096 * 256
@@ -120,8 +121,8 @@ def tile_hypconvhyperboloid_kernel(tc, x, W, b, out):
             tt = const.tile([P, 2 * COLW * 4], BF16, name="t%d" % pr, align_bytes=64)
             ts.append(tt)
         wg = const.tile([P, TAPS * OUT * 4], BF16, name="wg", align_bytes=64)
-        wc = const.tile([P, TAPS * OUT], U32, name="wc", align_bytes=64)
-        ws = const.tile([P, TAPS * OUT], U8, name="ws", align_bytes=64)
+        wc = const.tile([P, TAPS * OUT], U32, name="wc", align_bytes=256)
+        ws = const.tile([P, TAPS * OUT], U8, name="ws", align_bytes=256)
         state = {}
 
         def x_words(col, u):
@@ -222,8 +223,8 @@ def tile_hypconvhyperboloid_kernel(tc, x, W, b, out):
             return (q == 1 and n % 3 == 0) or (q == NQ - 1 and n % 3 == 2)
 
         def quant(q):
-            cod = codes.tile([P, TAPS * P], U32, tag="cod", name="cod", align_bytes=64)
-            scl = codes.tile([P, TAPS * P], U8, tag="scl", name="scl", align_bytes=64)
+            cod = codes.tile([P, SHIFT + TAPS * P], U32, tag="cod", name="cod", align_bytes=256)
+            scl = codes.tile([P, TAPS * 256], U8, tag="scl", name="scl", align_bytes=256)
             state["cod%d" % q] = cod
             state["scl%d" % q] = scl
             for n in range(TAPS):
@@ -233,8 +234,8 @@ def tile_hypconvhyperboloid_kernel(tc, x, W, b, out):
                 pr, k = divmod(min(max(q + j - 1, 0), NQ - 1), 2)
                 base = (k * COLW + i * 8) * 4
                 nc.vector.quantize_mx(
-                    out=cod[:, n * P : (n + 1) * P].bitcast(FP8X4),
-                    scales=scl[:, n * P : (n + 1) * P],
+                    out=cod[:, SHIFT + n * P : SHIFT + (n + 1) * P].bitcast(FP8X4),
+                    scales=scl[:, n * 256 : n * 256 + P],
                     in_=ts[pr][:, base : base + 512],
                 )
 
@@ -248,8 +249,8 @@ def tile_hypconvhyperboloid_kernel(tc, x, W, b, out):
                 s = SLOT[n]
                 nc.tensor.matmul_mx(
                     out=z[:, half * OUT : (half + 1) * OUT],
-                    lhsT=state["cod%d" % src][:, n * P : (n + 1) * P].bitcast(FP8X4),
-                    lhsT_scale=state["scl%d" % src][:, n * P : (n + 1) * P],
+                    lhsT=state["cod%d" % src][:, SHIFT + n * P : SHIFT + (n + 1) * P].bitcast(FP8X4),
+                    lhsT_scale=state["scl%d" % src][:, n * 256 : n * 256 + P],
                     rhs=wc[:, s * OUT : (s + 1) * OUT].bitcast(FP8X4),
                     rhs_scale=ws[:, s * OUT : (s + 1) * OUT],
                     start=(n == 0),

@@ -22,7 +22,6 @@ COLW = ROWS * 8
 CHUNKS = (0, 5, 9, 17, 25, 32)
 BATCHES = ((0, 4), (4, 8), (8, 16), (16, 32))
 SLOT = (0, 4, 1, 5, 2, 6, 3, 7, 8)
-SHIFT = 48
 LAG = 2
 
 FLOPS = 2 * 4096 * 4096 * 256
@@ -33,7 +32,7 @@ def tile_hypconvhyperboloid_kernel(tc, x, W, b, out):
     with ExitStack() as ctx:
         ctx.enter_context(tc.manual_schedule())
         const = ctx.enter_context(tc.tile_pool(name="const", bufs=1))
-        codes = ctx.enter_context(tc.tile_pool(name="codes", bufs=8))
+        codes = ctx.enter_context(tc.tile_pool(name="codes", bufs=10))
         outs = ctx.enter_context(tc.tile_pool(name="outs", bufs=2))
         ps_tr = ctx.enter_context(tc.psum_pool(name="ps_tr", bufs=3))
         ps_misc = ctx.enter_context(tc.psum_pool(name="ps_misc", bufs=2))
@@ -121,8 +120,8 @@ def tile_hypconvhyperboloid_kernel(tc, x, W, b, out):
             tt = const.tile([P, 2 * COLW * 4], BF16, name="t%d" % pr, align_bytes=64)
             ts.append(tt)
         wg = const.tile([P, TAPS * OUT * 4], BF16, name="wg", align_bytes=64)
-        wc = const.tile([P, TAPS * OUT], U32, name="wc", align_bytes=256)
-        ws = const.tile([P, TAPS * OUT], U8, name="ws", align_bytes=256)
+        wc = const.tile([P, TAPS * OUT], U32, name="wc", align_bytes=64)
+        ws = const.tile([P, TAPS * OUT], U8, name="ws", align_bytes=64)
         state = {}
 
         def x_words(col, u):
@@ -223,8 +222,8 @@ def tile_hypconvhyperboloid_kernel(tc, x, W, b, out):
             return (q == 1 and n % 3 == 0) or (q == NQ - 1 and n % 3 == 2)
 
         def quant(q):
-            cod = codes.tile([P, SHIFT + TAPS * P], U32, tag="cod", name="cod", align_bytes=256)
-            scl = codes.tile([P, TAPS * 256], U8, tag="scl", name="scl", align_bytes=256)
+            cod = codes.tile([P, TAPS * P], U32, tag="cod", name="cod", align_bytes=64)
+            scl = codes.tile([P, TAPS * P], U8, tag="scl", name="scl", align_bytes=64)
             state["cod%d" % q] = cod
             state["scl%d" % q] = scl
             for n in range(TAPS):
@@ -234,8 +233,8 @@ def tile_hypconvhyperboloid_kernel(tc, x, W, b, out):
                 pr, k = divmod(min(max(q + j - 1, 0), NQ - 1), 2)
                 base = (k * COLW + i * 8) * 4
                 nc.vector.quantize_mx(
-                    out=cod[:, SHIFT + n * P : SHIFT + (n + 1) * P].bitcast(FP8X4),
-                    scales=scl[:, n * 256 : n * 256 + P],
+                    out=cod[:, n * P : (n + 1) * P].bitcast(FP8X4),
+                    scales=scl[:, n * P : (n + 1) * P],
                     in_=ts[pr][:, base : base + 512],
                 )
 
@@ -249,8 +248,8 @@ def tile_hypconvhyperboloid_kernel(tc, x, W, b, out):
                 s = SLOT[n]
                 nc.tensor.matmul_mx(
                     out=z[:, half * OUT : (half + 1) * OUT],
-                    lhsT=state["cod%d" % src][:, SHIFT + n * P : SHIFT + (n + 1) * P].bitcast(FP8X4),
-                    lhsT_scale=state["scl%d" % src][:, n * 256 : n * 256 + P],
+                    lhsT=state["cod%d" % src][:, n * P : (n + 1) * P].bitcast(FP8X4),
+                    lhsT_scale=state["scl%d" % src][:, n * P : (n + 1) * P],
                     rhs=wc[:, s * OUT : (s + 1) * OUT].bitcast(FP8X4),
                     rhs_scale=ws[:, s * OUT : (s + 1) * OUT],
                     start=(n == 0),
@@ -283,6 +282,12 @@ def tile_hypconvhyperboloid_kernel(tc, x, W, b, out):
                     in_=o[:].rearrange("p q c -> p (q c)"),
                 )
 
+        def bias_rows():
+            bps = ps_misc.tile([P, 512], F32, tag="misc", name="bps")
+            nc.tensor.matmul(out=bps[:, 0:OUT], lhsT=ones[:], rhs=brow[:], start=True, stop=True)
+            nc.scalar.copy(out=bbc[:, 0:OUT], in_=bps[:, 0:OUT])
+            nc.scalar.copy(out=bbc[:, OUT : 2 * OUT], in_=bps[:, 0:OUT])
+
         squares(0)
         transposes(0)
         sums(0)
@@ -299,46 +304,50 @@ def tile_hypconvhyperboloid_kernel(tc, x, W, b, out):
         for n in (0, 2, 4, 6):
             weight_tap(n)
         weight_quant(0, 4)
-        for n in (1, 3, 5, 7, 8):
+        weight_tap(1)
+        weight_tap(3)
+        squares(1)
+        for n in (5, 7, 8):
             weight_tap(n)
         weight_quant(4, 8)
         weight_quant(8, 9)
-        bps = ps_misc.tile([P, 512], F32, tag="misc", name="bps")
-        nc.tensor.matmul(out=bps[:, 0:OUT], lhsT=ones[:], rhs=brow[:], start=True, stop=True)
-        nc.scalar.copy(out=bbc[:, 0:OUT], in_=bps[:, 0:OUT])
-        nc.scalar.copy(out=bbc[:, OUT : 2 * OUT], in_=bps[:, 0:OUT])
-        squares(1)
-        squares(2)
         transposes(2)
         sums(1)
         transposes(3)
         copy_out(2, "a")
         roots(1)
         rows(1)
-        sums(2)
         row_write(2, "a")
+        passes(0)
         copy_out(3, "a")
         row_write(3, "a")
+        quant(3)
+        passes(1)
+        passes(2)
+        squares(2)
+        sums(2)
         roots(2)
+        bias_rows()
+        quant(4)
+        passes(3)
 
-        for blk in range(8):
-            g = blk + 2
+        for blk in range(1, 8):
+            g = blk + 1
             if g < 8:
-                if blk == 1:
-                    sums(3)
-                    roots(3)
                 transposes(2 * g)
                 transposes(2 * g + 1)
                 rows(g)
                 for pr in (2 * g, 2 * g + 1):
                     copy_out(pr, "a")
-                for pr in (2 * g, 2 * g + 1):
                     row_write(pr, "a")
-                if blk == 0:
+                if blk == 1:
                     squares(3)
                     squares(4)
+                if blk == 2:
+                    sums(3)
+                    roots(3)
             for q in range(4 * blk, 4 * blk + 4):
-                if q > 2:
+                if q > 4:
                     quant(q)
                 passes(q)
                 if q % 2 == 1 and q // 2 - LAG >= 0:

@@ -17,12 +17,15 @@ CH = 456
 CPAD = 512
 OUT = 256
 TAPS = 9
-ROWS = 18
-COLW = ROWS * 8
-CHUNKS = (0, 5, 9, 17, 25, 32)
-BATCHES = ((0, 4), (4, 8), (8, 16), (16, 32))
+WIN = 512
+NCOL = NQ + 2
+CHUNKS = (0, 6, 10, 18, 26, 32)
+NCHUNK = 5
+GROUPS = ((0, 2), (2, 2), (4, 4), (8, 4), (12, 4), (16, 4), (20, 4), (24, 4), (28, 2), (30, 2))
 SLOT = (0, 4, 1, 5, 2, 6, 3, 7, 8)
-LAG = 2
+ORDER = (3, 0, 6, 4, 1, 7, 5, 2, 8)
+RING = 22
+WOFF = 16 * WIN
 
 FLOPS = 2 * 4096 * 4096 * 256
 
@@ -32,36 +35,38 @@ def tile_hypconvhyperboloid_kernel(tc, x, W, b, out):
     with ExitStack() as ctx:
         ctx.enter_context(tc.manual_schedule())
         const = ctx.enter_context(tc.tile_pool(name="const", bufs=1))
-        codes = ctx.enter_context(tc.tile_pool(name="codes", bufs=10))
+        codes = ctx.enter_context(tc.tile_pool(name="codes", bufs=RING))
         outs = ctx.enter_context(tc.tile_pool(name="outs", bufs=2))
         ps_tr = ctx.enter_context(tc.psum_pool(name="ps_tr", bufs=3))
-        ps_misc = ctx.enter_context(tc.psum_pool(name="ps_misc", bufs=2))
-        ps_z = ctx.enter_context(tc.psum_pool(name="ps_z", bufs=3))
+        ps_misc = ctx.enter_context(tc.psum_pool(name="ps_misc", bufs=1))
+        ps_z = ctx.enter_context(tc.psum_pool(name="ps_z", bufs=4))
 
         x_rows = x.rearrange("b r q c -> (b r) q c")
         out_rows = out.rearrange("b (h l) q c -> l (b h) (q c)", h=2, l=16)
 
         xs = []
-        for c in range(5):
+        for c in range(NCHUNK):
             xt = const.tile([P, (CHUNKS[c + 1] - CHUNKS[c]) * CPAD], BF16, name="x%d" % c)
             xs.append(xt)
-        wts = []
-        for ot in range(2):
-            wt = const.tile([P, TAPS * CPAD], BF16, name="wt%d" % ot)
-            wts.append(wt)
-        wvs = [wts[ot][:].rearrange("p (n c) -> p n c", c=CPAD) for ot in range(2)]
+        xvs = [xs[c][:].rearrange("p (k c) -> p k c", c=CPAD) for c in range(NCHUNK)]
+        wins = []
+        for i in range(3):
+            wt = const.tile([P, NCOL * WIN], BF16, name="win%d" % i, align_bytes=64)
+            wins.append(wt)
+        wraw = [wins[0][:, WOFF + ot * TAPS * CPAD : WOFF + (ot + 1) * TAPS * CPAD] for ot in range(2)]
+        wvs = [wraw[ot].rearrange("p (n c) -> p n c", c=CPAD) for ot in range(2)]
+        wg = wins[1][:, WOFF : WOFF + TAPS * OUT * 4]
 
         def load_x(c):
-            xv = xs[c][:].rearrange("p (k c) -> p k c", c=CPAD)
-            nc.vector.memset(xv[:, :, 448:CPAD], 0.0)
-            nc.sync.dma_start(out=xv[:, :, 0:CH], in_=x_rows[:, CHUNKS[c] : CHUNKS[c + 1], :])
+            nc.vector.memset(xvs[c][:, :, CH:CPAD], 0.0)
+            nc.sync.dma_start(out=xvs[c][:, :, 0:CH], in_=x_rows[:, CHUNKS[c] : CHUNKS[c + 1], :])
 
         brow = const.tile([P, OUT], BF16, name="brow")
         nc.vector.memset(brow[:], 0.0)
         nc.scalar.dma_start(out=brow[0:1, :], in_=b.unsqueeze(0))
         load_x(0)
         for ot in range(2):
-            nc.vector.memset(wvs[ot][:, :, 448:CPAD], 0.0)
+            nc.vector.memset(wvs[ot][:, :, CH:CPAD], 0.0)
         for ot in range(2):
             nc.sync.dma_start(
                 out=wvs[ot][:, 0:8:2, 0:CH],
@@ -74,7 +79,7 @@ def tile_hypconvhyperboloid_kernel(tc, x, W, b, out):
             )
         for ot in range(2):
             nc.sync.dma_start(out=wvs[ot][:, 8, 0:CH], in_=W[ot * P : (ot + 1) * P, 3640:4096])
-        for c in range(1, 5):
+        for c in range(1, NCHUNK):
             load_x(c)
 
         one1 = const.tile([P, 1], F32, name="one1")
@@ -98,8 +103,6 @@ def tile_hypconvhyperboloid_kernel(tc, x, W, b, out):
         nc.vector.tensor_tensor(out=bv[:, :, 1:32], in0=bv[:, :, 1:32], in1=iv[:, :, 0:31], op=ALU.add)
         nc.vector.tensor_tensor(out=bv[:, :, 0:31], in0=bv[:, :, 0:31], in1=iv[:, :, 1:32], op=ALU.add)
         nc.vector.tensor_tensor(out=bv[:, :, 0:32:31], in0=bv[:, :, 0:32:31], in1=iv[:, :, 0:32:31], op=ALU.add)
-        permb = const.tile([P, P], BF16, name="permb")
-        nc.vector.tensor_copy(out=permb[:], in_=permf[:])
         ones = const.tile([P, P], BF16, name="ones")
         nc.vector.memset(ones[:], 1.0)
 
@@ -114,56 +117,27 @@ def tile_hypconvhyperboloid_kernel(tc, x, W, b, out):
 
         bbc = const.tile([P, 2 * OUT], F32, name="bbc")
         sq = const.tile([P, NQ + 2], F32, name="sq")
-        tcat = const.tile([P, NQ], BF16, name="tcat")
-        ts = []
-        for pr in range(NQ // 2):
-            tt = const.tile([P, 2 * COLW * 4], BF16, name="t%d" % pr, align_bytes=64)
-            ts.append(tt)
-        wg = const.tile([P, TAPS * OUT * 4], BF16, name="wg", align_bytes=64)
         wc = const.tile([P, TAPS * OUT], U32, name="wc", align_bytes=64)
         ws = const.tile([P, TAPS * OUT], U8, name="ws", align_bytes=64)
         state = {}
 
+        def batch(bt):
+            return max(CHUNKS[bt] - 1, 0), (CHUNKS[bt + 1] - 1 if bt < NCHUNK - 1 else NQ)
+
         def x_words(col, u):
-            c = max(i for i in range(5) if CHUNKS[i] <= col)
+            c = max(i for i in range(NCHUNK) if CHUNKS[i] <= col)
             xf = xs[c][:].bitcast(F32).rearrange("p (k w u) -> p k w u", w=P, u=2)
             return xf[:, col - CHUNKS[c], :, u]
 
         def squares(c):
-            xv = xs[c][:].rearrange("p (k c) -> p k c", c=CPAD)
-            nc.scalar.activation(out=sq[:, 1 + CHUNKS[c] : 1 + CHUNKS[c + 1]], in_=xv[:, :, 0], func=ACT.Square)
+            nc.scalar.activation(out=sq[:, 1 + CHUNKS[c] : 1 + CHUNKS[c + 1]], in_=xvs[c][:, :, 0], func=ACT.Square)
             if c == 0:
                 nc.scalar.copy(out=sq[:, 0:1], in_=sq[:, 1:2])
-            if c == 4:
+            if c == NCHUNK - 1:
                 nc.scalar.copy(out=sq[:, NQ + 1 : NQ + 2], in_=sq[:, NQ : NQ + 1])
 
-        def transposes(pr):
-            tr = ps_tr.tile([P, 512], F32, tag="tr", name="tr")
-            for k in range(2):
-                for u in range(2):
-                    s = 2 * k + u
-                    nc.tensor.transpose(tr[:, s * P : (s + 1) * P], x_words(2 * pr + k, u), permf[:])
-            state["tr%d" % pr] = tr
-
-        def copy_on(eng, dst, src):
-            if eng == "v":
-                nc.vector.tensor_copy(out=dst, in_=src)
-            else:
-                nc.scalar.copy(out=dst, in_=src)
-
-        def copy_out(pr, eng):
-            t32 = ts[pr][:].bitcast(F32)
-            copy_on(
-                eng,
-                t32.rearrange("p (k w) -> p k w", w=COLW * 2)[:, :, 16:272].rearrange("p k (w u) -> p k w u", u=2),
-                state["tr%d" % pr][:].rearrange("p (k u w) -> p k w u", k=2, u=2),
-            )
-            t6 = t32.rearrange("p (k r b h u) -> p k r b h u", r=ROWS, b=4, h=2, u=2)
-            for dst, hs in ((0, 0), (ROWS - 1, 1)):
-                copy_on(eng, t6[:, :, dst, :, :, :], t6[:, :, 1:17:15, :, hs, :].rearrange("p k r b u -> p k b r u"))
-
         def sums(bt):
-            lo, hi = BATCHES[bt]
+            lo, hi = batch(bt)
             sps = ps_misc.tile([P, 512], F32, tag="misc", name="sps")
             for j in range(3):
                 nc.tensor.matmul(
@@ -172,37 +146,51 @@ def tile_hypconvhyperboloid_kernel(tc, x, W, b, out):
             state["sps%d" % bt] = sps
 
         def roots(bt):
-            lo, hi = BATCHES[bt]
-            nc.scalar.activation(
-                out=tcat[:, lo:hi], in_=state["sps%d" % bt][:, 0 : hi - lo], func=ACT.Sqrt, bias=neg8[:], scale=1.0
-            )
+            lo, hi = batch(bt)
+            for c in range(NCHUNK):
+                a, e = max(lo, CHUNKS[c]), min(hi, CHUNKS[c + 1])
+                if a < e:
+                    nc.scalar.activation(
+                        out=xvs[c][:, a - CHUNKS[c] : e - CHUNKS[c], 0],
+                        in_=state["sps%d" % bt][:, a - lo : e - lo],
+                        func=ACT.Sqrt,
+                        bias=neg8[:],
+                        scale=1.0,
+                    )
 
-        def rows(g):
-            rw = ps_misc.tile([P, 512], F32, tag="misc", name="rw")
-            for k in range(4):
-                nc.tensor.matmul(
-                    out=rw[:, k * P : (k + 1) * P],
-                    lhsT=tcat[:, 4 * g + k : 4 * g + k + 1].to_broadcast([P, P]),
-                    rhs=permb[:],
-                    start=True,
-                    stop=True,
-                )
-            state["rw%d" % g] = rw
+        def transposes(pp):
+            tr = ps_tr.tile([P, 512], F32, tag="tr", name="tr")
+            for k in range(2):
+                col = min(max(2 * pp - 1 + k, 0), NQ - 1)
+                for u in range(2):
+                    s = 2 * k + u
+                    nc.tensor.transpose(tr[:, s * P : (s + 1) * P], x_words(col, u), permf[:])
+            state["tr%d" % pp] = tr
 
-        def row_write(pr, eng):
-            tv = ts[pr][:].rearrange("p (k w t) -> p k w t", w=COLW, t=4)
-            half = pr % 2
-            copy_on(
-                eng,
-                tv[0:1, :, 8:136, 0],
-                state["rw%d" % (pr // 2)][0:1, half * 256 : (half + 1) * 256].rearrange("p (k w) -> p k w", k=2),
-            )
+        def copy_on(eng, dst, src):
+            if eng == "v":
+                nc.vector.tensor_copy(out=dst, in_=src)
+            else:
+                nc.scalar.copy(out=dst, in_=src)
+
+        def stage(pp, eng):
+            tr = state["tr%d" % pp]
+            src = tr[:].rearrange("p (k u w) -> p k w u", k=2, u=2)
+            src6 = tr[:].rearrange("p (k u l b h) -> p k u l b h", k=2, u=2, l=16, b=4)
+            d32 = [wins[i][:, 2 * pp * WIN : (2 * pp + 2) * WIN].bitcast(F32) for i in range(3)]
+            dst = [d32[i].rearrange("p (k w u) -> p k w u", k=2, u=2) for i in range(3)]
+            dst6 = [d32[i].rearrange("p (k l b h u) -> p k l b h u", k=2, l=16, b=4, h=2) for i in range(3)]
+            copy_on(eng, dst[1], src)
+            copy_on(eng, dst[0][:, :, 8:P, :], src[:, :, 0 : P - 8, :])
+            copy_on(eng, dst6[0][:, :, 0, :, :, :], src6[:, :, :, 0:16:15, :, 0].rearrange("p k u l b -> p k b l u"))
+            copy_on(eng, dst[2][:, :, 0 : P - 8, :], src[:, :, 8:P, :])
+            copy_on(eng, dst6[2][:, :, 15, :, :, :], src6[:, :, :, 0:16:15, :, 1].rearrange("p k u l b -> p k b l u"))
 
         def weight_tap(n):
-            wg32 = wg[:].bitcast(F32)
-            tr = ps_tr.tile([P, 512], F32, tag="tr", name="trw")
+            wg32 = wg.bitcast(F32)
+            tr = ps_z.tile([P, 512], F32, tag="z", name="trw")
             for ot in range(2):
-                wf = wts[ot][:].bitcast(F32).rearrange("p (n w u) -> p n w u", w=P, u=2)
+                wf = wraw[ot].bitcast(F32).rearrange("p (n w u) -> p n w u", w=P, u=2)
                 for u in range(2):
                     s = 2 * ot + u
                     nc.tensor.transpose(tr[:, s * P : (s + 1) * P], wf[:, n, :, u], ident[:])
@@ -218,57 +206,54 @@ def tile_hypconvhyperboloid_kernel(tc, x, W, b, out):
                 in_=wg[:, s0 * OUT * 4 : s1 * OUT * 4],
             )
 
-        def shared(q, n):
-            return (q == 1 and n % 3 == 0) or (q == NQ - 1 and n % 3 == 2)
+        def quant(gi, n):
+            q0, width = GROUPS[gi]
+            i, j = divmod(n, 3)
+            cod = codes.tile([P, width * P], U32, tag="cod", name="cod", align_bytes=64)
+            scl = codes.tile([P, width * P], U8, tag="scl", name="scl", align_bytes=64)
+            state[("cod", gi, n)] = cod
+            state[("scl", gi, n)] = scl
+            nc.vector.quantize_mx(
+                out=cod[:].bitcast(FP8X4),
+                scales=scl[:],
+                in_=wins[i][:, (q0 + j) * WIN : (q0 + j + width) * WIN],
+            )
 
-        def quant(q):
-            cod = codes.tile([P, TAPS * P], U32, tag="cod", name="cod", align_bytes=64)
-            scl = codes.tile([P, TAPS * P], U8, tag="scl", name="scl", align_bytes=64)
-            state["cod%d" % q] = cod
-            state["scl%d" % q] = scl
-            for n in range(TAPS):
-                if shared(q, n):
-                    continue
-                i, j = divmod(n, 3)
-                pr, k = divmod(min(max(q + j - 1, 0), NQ - 1), 2)
-                base = (k * COLW + i * 8) * 4
-                nc.vector.quantize_mx(
-                    out=cod[:, n * P : (n + 1) * P].bitcast(FP8X4),
-                    scales=scl[:, n * P : (n + 1) * P],
-                    in_=ts[pr][:, base : base + 512],
-                )
-
-        def passes(q):
+        def passes(gi, q):
+            q0 = GROUPS[gi][0]
             half = q % 2
             if half == 0:
                 state["z%d" % (q // 2)] = ps_z.tile([P, 512], F32, tag="z", name="z")
             z = state["z%d" % (q // 2)]
-            for n in range(TAPS):
-                src = q - 1 if shared(q, n) else q
+            w0 = (q - q0) * P
+            for n in ORDER:
                 s = SLOT[n]
                 nc.tensor.matmul_mx(
                     out=z[:, half * OUT : (half + 1) * OUT],
-                    lhsT=state["cod%d" % src][:, n * P : (n + 1) * P].bitcast(FP8X4),
-                    lhsT_scale=state["scl%d" % src][:, n * P : (n + 1) * P],
+                    lhsT=state[("cod", gi, n)][:, w0 : w0 + P].bitcast(FP8X4),
+                    lhsT_scale=state[("scl", gi, n)][:, w0 : w0 + P],
                     rhs=wc[:, s * OUT : (s + 1) * OUT].bitcast(FP8X4),
                     rhs_scale=ws[:, s * OUT : (s + 1) * OUT],
-                    start=(n == 0),
-                    stop=(n == TAPS - 1),
+                    start=(n == ORDER[0]),
+                    stop=(n == ORDER[TAPS - 1]),
                 )
 
-        def finish(pp):
+        def finish_add(pp):
             s = (2 * pp) % 8
             if s == 0:
                 state["o"] = outs.tile([P, 8, OUT + 1], F32, tag="o", name="o")
                 state["ss"] = outs.tile([P, 8], F32, tag="ss", name="ss")
-            o = state["o"]
-            ss = state["ss"]
             nc.vector.tensor_tensor(
-                out=o[:, s : s + 2, 1 : OUT + 1],
+                out=state["o"][:, s : s + 2, 1 : OUT + 1],
                 in0=state["z%d" % pp][:].rearrange("p (k n) -> p k n", k=2),
                 in1=bbc[:].rearrange("p (k n) -> p k n", k=2),
                 op=ALU.add,
             )
+
+        def finish_squares(pp):
+            s = (2 * pp) % 8
+            o = state["o"]
+            ss = state["ss"]
             for k in (s, s + 1):
                 junk = outs.tile([P, OUT], BF16, tag="junk", name="junk")
                 nc.scalar.activation(
@@ -288,69 +273,57 @@ def tile_hypconvhyperboloid_kernel(tc, x, W, b, out):
             nc.scalar.copy(out=bbc[:, 0:OUT], in_=bps[:, 0:OUT])
             nc.scalar.copy(out=bbc[:, OUT : 2 * OUT], in_=bps[:, 0:OUT])
 
+        def last_pair(gi):
+            return (GROUPS[gi][0] + GROUPS[gi][1] + 1) // 2
+
         squares(0)
-        transposes(0)
         sums(0)
-        copy_out(0, "a")
         roots(0)
+        transposes(0)
         transposes(1)
-        rows(0)
-        row_write(0, "a")
-        copy_out(1, "v")
-        row_write(1, "v")
-        quant(0)
-        quant(1)
-        quant(2)
+        transposes(2)
+        stage(0, "v")
+        stage(1, "a")
+        stage(2, "v")
         for n in (0, 2, 4, 6):
             weight_tap(n)
+        for n in ORDER:
+            quant(0, n)
         weight_quant(0, 4)
-        weight_tap(1)
-        weight_tap(3)
-        squares(1)
-        for n in (5, 7, 8):
+        for n in (1, 3, 5, 7):
             weight_tap(n)
         weight_quant(4, 8)
+        weight_tap(8)
         weight_quant(8, 9)
-        transposes(2)
-        sums(1)
-        transposes(3)
-        copy_out(2, "a")
-        roots(1)
-        rows(1)
-        row_write(2, "a")
-        passes(0)
-        copy_out(3, "a")
-        row_write(3, "a")
-        quant(3)
-        passes(1)
-        passes(2)
-        squares(2)
-        sums(2)
-        roots(2)
         bias_rows()
-        quant(4)
-        passes(3)
+        squares(1)
+        sums(1)
+        roots(1)
 
-        for blk in range(1, 8):
-            g = blk + 1
-            if g < 8:
-                transposes(2 * g)
-                transposes(2 * g + 1)
-                rows(g)
-                for pr in (2 * g, 2 * g + 1):
-                    copy_out(pr, "a")
-                    row_write(pr, "a")
-                if blk == 1:
-                    squares(3)
-                    squares(4)
-                if blk == 2:
-                    sums(3)
-                    roots(3)
-            for q in range(4 * blk, 4 * blk + 4):
-                if q > 4:
-                    quant(q)
-                passes(q)
-                if q % 2 == 1 and q // 2 - LAG >= 0:
-                    finish(q // 2 - LAG)
-        for pp in range(NQ // 2 - LAG, NQ // 2):
-            finish(pp)
+        groups = len(GROUPS)
+        staged = 3
+        for gi in range(groups):
+            q0, width = GROUPS[gi]
+            new = []
+            if gi + 2 < groups:
+                new = list(range(staged, last_pair(gi + 2) + 1))
+                staged = last_pair(gi + 2) + 1
+            bt = gi + 2
+            for pp in new:
+                transposes(pp)
+            for m, pp in enumerate(new):
+                stage(pp, "a")
+                if m == 0 and bt < NCHUNK:
+                    squares(bt)
+            calls = ORDER if gi + 1 < groups else ()
+            parts = width // 2
+            for m in range(parts):
+                passes(gi, q0 + 2 * m)
+                passes(gi, q0 + 2 * m + 1)
+                if m == 0 and bt < NCHUNK:
+                    sums(bt)
+                    roots(bt)
+                for n in calls[m * TAPS // parts : (m + 1) * TAPS // parts]:
+                    quant(gi + 1, n)
+                finish_add(q0 // 2 + m)
+                finish_squares(q0 // 2 + m)

@@ -23,7 +23,9 @@ CHUNKS = (0, 6, 10, 18, 26, 32)
 NCHUNK = 5
 GROUPS = ((0, 2), (2, 2), (4, 4), (8, 4), (12, 4), (16, 4), (20, 4), (24, 4), (28, 2), (30, 2))
 SLOT = (0, 4, 1, 5, 2, 6, 3, 7, 8)
-ORDER = (3, 0, 6, 4, 1, 7, 5, 2, 8)
+CALLS = (0, 6, 4, 1, 7, 5, 2, 8)
+LENT = 3
+ORDER = (LENT,) + CALLS
 RING = 22
 WOFF = 16 * WIN
 
@@ -225,13 +227,17 @@ def tile_hypconvhyperboloid_kernel(tc, x, W, b, out):
             if half == 0:
                 state["z%d" % (q // 2)] = ps_z.tile([P, 512], F32, tag="z", name="z")
             z = state["z%d" % (q // 2)]
-            w0 = (q - q0) * P
             for n in ORDER:
                 s = SLOT[n]
+                src, w0 = (gi, n), (q - q0) * P
+                if n == LENT:
+                    left = max(q - 1, 0)
+                    gl = gi if left >= q0 else gi - 1
+                    src, w0 = (gl, LENT + 1), (left - GROUPS[gl][0]) * P
                 nc.tensor.matmul_mx(
                     out=z[:, half * OUT : (half + 1) * OUT],
-                    lhsT=state[("cod", gi, n)][:, w0 : w0 + P].bitcast(FP8X4),
-                    lhsT_scale=state[("scl", gi, n)][:, w0 : w0 + P],
+                    lhsT=state[("cod",) + src][:, w0 : w0 + P].bitcast(FP8X4),
+                    lhsT_scale=state[("scl",) + src][:, w0 : w0 + P],
                     rhs=wc[:, s * OUT : (s + 1) * OUT].bitcast(FP8X4),
                     rhs_scale=ws[:, s * OUT : (s + 1) * OUT],
                     start=(n == ORDER[0]),
@@ -287,7 +293,7 @@ def tile_hypconvhyperboloid_kernel(tc, x, W, b, out):
         stage(2, "v")
         for n in (0, 2, 4, 6):
             weight_tap(n)
-        for n in ORDER:
+        for n in CALLS:
             quant(0, n)
         weight_quant(0, 4)
         for n in (1, 3, 5, 7):
@@ -302,6 +308,7 @@ def tile_hypconvhyperboloid_kernel(tc, x, W, b, out):
 
         groups = len(GROUPS)
         staged = 3
+        pending = []
         for gi in range(groups):
             q0, width = GROUPS[gi]
             new = []
@@ -315,15 +322,21 @@ def tile_hypconvhyperboloid_kernel(tc, x, W, b, out):
                 stage(pp, "a")
                 if m == 0 and bt < NCHUNK:
                     squares(bt)
-            calls = ORDER if gi + 1 < groups else ()
+            calls = CALLS if gi + 1 < groups else ()
             parts = width // 2
             for m in range(parts):
+                for n in calls[m * len(calls) // parts : (m + 1) * len(calls) // parts]:
+                    quant(gi + 1, n)
+                if pending:
+                    finish_add(pending[0])
+                    finish_squares(pending[0])
+                    pending.remove(pending[0])
                 passes(gi, q0 + 2 * m)
                 passes(gi, q0 + 2 * m + 1)
+                pending.append(q0 // 2 + m)
                 if m == 0 and bt < NCHUNK:
                     sums(bt)
                     roots(bt)
-                for n in calls[m * TAPS // parts : (m + 1) * TAPS // parts]:
-                    quant(gi + 1, n)
-                finish_add(q0 // 2 + m)
-                finish_squares(q0 // 2 + m)
+        for pp in pending:
+            finish_add(pp)
+            finish_squares(pp)

@@ -22,12 +22,13 @@ NCOL = NQ + 2
 CHUNKS = (0, 6, 10, 18, 26, 32)
 NCHUNK = 5
 GROUPS = ((0, 2), (2, 2), (4, 4), (8, 4), (12, 4), (16, 4), (20, 4), (24, 4), (28, 2), (30, 2))
-SLOT = (0, 4, 1, 5, 2, 6, 3, 7, 8)
 CALLS = (0, 6, 4, 1, 7, 5, 2, 8)
 LENT = 3
 ORDER = (LENT,) + CALLS
 RING = 22
 WOFF = 16 * WIN
+ALONE = NQ - 2
+CUT = (ALONE % 8) * (OUT + 1) // 8 * 8
 
 FLOPS = 2 * 4096 * 4096 * 256
 
@@ -55,8 +56,9 @@ def tile_hypconvhyperboloid_kernel(tc, x, W, b, out):
         for i in range(3):
             wt = const.tile([P, NCOL * WIN], BF16, name="win%d" % i, align_bytes=64)
             wins.append(wt)
-        wraw = [wins[0][:, WOFF + ot * TAPS * CPAD : WOFF + (ot + 1) * TAPS * CPAD] for ot in range(2)]
-        wvs = [wraw[ot].rearrange("p (n c) -> p n c", c=CPAD) for ot in range(2)]
+        wraw = wins[0][:, WOFF : WOFF + 2 * TAPS * CPAD]
+        wv = wraw.rearrange("p (n t c) -> p n t c", t=2, c=CPAD)
+        w_taps = W.rearrange("(t o) k -> o t k", t=2)
         wg = wins[1][:, WOFF : WOFF + TAPS * OUT * 4]
 
         def load_x(c):
@@ -67,22 +69,20 @@ def tile_hypconvhyperboloid_kernel(tc, x, W, b, out):
         nc.vector.memset(brow[:], 0.0)
         nc.scalar.dma_start(out=brow[0:1, :], in_=b.unsqueeze(0))
         load_x(0)
-        for ot in range(2):
-            nc.vector.memset(wvs[ot][:, :, CH:CPAD], 0.0)
-        for ot in range(2):
-            nc.sync.dma_start(
-                out=wvs[ot][:, 0:8:2, 0:CH],
-                in_=W[ot * P : (ot + 1) * P, 0:3640].rearrange("o (m c) -> o m c", c=910)[:, :, 0:CH],
-            )
-        for ot in range(2):
-            nc.sync.dma_start(
-                out=wvs[ot][:, 1:8:2, 0:CH],
-                in_=W[ot * P : (ot + 1) * P, 455:4095].rearrange("o (m c) -> o m c", c=910)[:, :, 0:CH],
-            )
-        for ot in range(2):
-            nc.sync.dma_start(out=wvs[ot][:, 8, 0:CH], in_=W[ot * P : (ot + 1) * P, 3640:4096])
-        for c in range(1, NCHUNK):
-            load_x(c)
+        nc.vector.memset(wv[:, :, :, CH:CPAD], 0.0)
+        nc.sync.dma_start(out=wv[:, 0, :, 0:CH], in_=w_taps[:, :, 455 * 0 : 455 * 0 + CH])
+        nc.sync.dma_start(out=wv[:, 1, :, 0:CH], in_=w_taps[:, :, 455 * 1 : 455 * 1 + CH])
+        nc.sync.dma_start(out=wv[:, 2, :, 0:CH], in_=w_taps[:, :, 455 * 2 : 455 * 2 + CH])
+        nc.sync.dma_start(out=wv[:, 3, :, 0:CH], in_=w_taps[:, :, 455 * 3 : 455 * 3 + CH])
+        nc.sync.dma_start(out=wv[:, 4, :, 0:CH], in_=w_taps[:, :, 455 * 4 : 455 * 4 + CH])
+        load_x(1)
+        nc.sync.dma_start(out=wv[:, 5, :, 0:CH], in_=w_taps[:, :, 455 * 5 : 455 * 5 + CH])
+        nc.sync.dma_start(out=wv[:, 6, :, 0:CH], in_=w_taps[:, :, 455 * 6 : 455 * 6 + CH])
+        nc.sync.dma_start(out=wv[:, 7, :, 0:CH], in_=w_taps[:, :, 455 * 7 : 455 * 7 + CH])
+        nc.sync.dma_start(out=wv[:, 8, :, 0:CH], in_=w_taps[:, :, 455 * 8 : 455 * 8 + CH])
+        load_x(2)
+        load_x(3)
+        load_x(4)
 
         one1 = const.tile([P, 1], F32, name="one1")
         nc.vector.memset(one1[:], 1.0)
@@ -108,14 +108,13 @@ def tile_hypconvhyperboloid_kernel(tc, x, W, b, out):
         ones = const.tile([P, P], BF16, name="ones")
         nc.vector.memset(ones[:], 1.0)
 
-        for ot in range(2):
-            nc.gpsimd.tensor_copy(out=wvs[ot][:, 4, 0:1], in_=wvs[ot][:, 0, 0:1])
-            nc.gpsimd.memset(wvs[ot][:, 0:4:2, 0:1], 0.0)
-            nc.gpsimd.memset(wvs[ot][:, 6:7, 0:1], 0.0)
-        for ot in range(2):
-            nc.gpsimd.memset(wvs[ot][:, 1:8:2, 0:1], 0.0)
-        for ot in range(2):
-            nc.gpsimd.memset(wvs[ot][:, 8:9, 0:1], 0.0)
+        wfirst = const.tile([P, 2], BF16, name="wfirst")
+        nc.gpsimd.tensor_copy(out=wfirst[:], in_=wv[:, 0, :, 0])
+        for n in range(TAPS):
+            if n == 4:
+                nc.gpsimd.tensor_copy(out=wv[:, n, :, 0], in_=wfirst[:])
+            else:
+                nc.gpsimd.memset(wv[:, n, :, 0], 0.0)
 
         bbc = const.tile([P, 2 * OUT], F32, name="bbc")
         sq = const.tile([P, NQ + 2], F32, name="sq")
@@ -188,17 +187,18 @@ def tile_hypconvhyperboloid_kernel(tc, x, W, b, out):
             copy_on(eng, dst[2][:, :, 0 : P - 8, :], src[:, :, 8:P, :])
             copy_on(eng, dst6[2][:, :, 15, :, :, :], src6[:, :, :, 0:16:15, :, 1].rearrange("p k u l b -> p k b l u"))
 
-        def weight_tap(n):
+        def weight_tap(n, eng="a"):
             wg32 = wg.bitcast(F32)
             tr = ps_z.tile([P, 512], F32, tag="z", name="trw")
+            wf = wraw.bitcast(F32).rearrange("p (n t w u) -> p n t w u", t=2, w=P, u=2)
             for ot in range(2):
-                wf = wraw[ot].bitcast(F32).rearrange("p (n w u) -> p n w u", w=P, u=2)
                 for u in range(2):
                     s = 2 * ot + u
-                    nc.tensor.transpose(tr[:, s * P : (s + 1) * P], wf[:, n, :, u], ident[:])
-            nc.scalar.copy(
-                out=wg32[:, SLOT[n] * 512 : (SLOT[n] + 1) * 512].rearrange("p (t o u) -> p t o u", t=2, u=2),
-                in_=tr[:].rearrange("p (t u o) -> p t o u", t=2, u=2),
+                    nc.tensor.transpose(tr[:, s * P : (s + 1) * P], wf[:, n, ot, :, u], ident[:])
+            copy_on(
+                eng,
+                wg32[:, n * 512 : (n + 1) * 512].rearrange("p (t o u) -> p t o u", t=2, u=2),
+                tr[:].rearrange("p (t u o) -> p t o u", t=2, u=2),
             )
 
         def weight_quant(s0, s1):
@@ -223,12 +223,12 @@ def tile_hypconvhyperboloid_kernel(tc, x, W, b, out):
 
         def passes(gi, q):
             q0 = GROUPS[gi][0]
-            half = q % 2
+            half = q % 2 if q < ALONE else 0
             if half == 0:
-                state["z%d" % (q // 2)] = ps_z.tile([P, 512], F32, tag="z", name="z")
-            z = state["z%d" % (q // 2)]
+                state["z%d" % q] = ps_z.tile([P, 512], F32, tag="z", name="z")
+            z = state["z%d" % (q - half)]
             for n in ORDER:
-                s = SLOT[n]
+                s = n
                 src, w0 = (gi, n), (q - q0) * P
                 if n == LENT:
                     left = max(q - 1, 0)
@@ -244,33 +244,36 @@ def tile_hypconvhyperboloid_kernel(tc, x, W, b, out):
                     stop=(n == ORDER[TAPS - 1]),
                 )
 
-        def finish_add(pp):
-            s = (2 * pp) % 8
+        def finish_add(q, n):
+            s = q % 8
             if s == 0:
                 state["o"] = outs.tile([P, 8, OUT + 1], F32, tag="o", name="o")
                 state["ss"] = outs.tile([P, 8], F32, tag="ss", name="ss")
             nc.vector.tensor_tensor(
-                out=state["o"][:, s : s + 2, 1 : OUT + 1],
-                in0=state["z%d" % pp][:].rearrange("p (k n) -> p k n", k=2),
-                in1=bbc[:].rearrange("p (k n) -> p k n", k=2),
+                out=state["o"][:, s : s + n, 1 : OUT + 1],
+                in0=state["z%d" % q][:, 0 : n * OUT].rearrange("p (k n) -> p k n", k=n),
+                in1=bbc[:, 0 : n * OUT].rearrange("p (k n) -> p k n", k=n),
                 op=ALU.add,
             )
 
-        def finish_squares(pp):
-            s = (2 * pp) % 8
+        def finish_squares(q, n):
+            s = q % 8
             o = state["o"]
             ss = state["ss"]
-            for k in (s, s + 1):
+            for k in range(s, s + n):
                 junk = outs.tile([P, OUT], BF16, tag="junk", name="junk")
                 nc.scalar.activation(
                     out=junk[:], in_=o[:, k, 1 : OUT + 1], func=ACT.Square, accum_out=ss[:, k : k + 1]
                 )
-            if s == 6:
-                q0 = 2 * pp - 6
-                nc.scalar.activation(out=o[:, :, 0], in_=ss[:], func=ACT.Sqrt, bias=one1[:], scale=1.0)
+            done = q + n
+            if done % 8 == 0 or done == ALONE:
+                k0, f0 = (ALONE % 8, CUT) if done == NQ else (0, 0)
+                k1, f1 = (ALONE % 8, CUT) if done == ALONE else (8, 8 * (OUT + 1))
+                base = (done - 1) // 8 * 8 * (OUT + 1)
+                nc.scalar.activation(out=o[:, k0:k1, 0], in_=ss[:, k0:k1], func=ACT.Sqrt, bias=one1[:], scale=1.0)
                 nc.sync.dma_start(
-                    out=out_rows[:, :, q0 * (OUT + 1) : (q0 + 8) * (OUT + 1)],
-                    in_=o[:].rearrange("p q c -> p (q c)"),
+                    out=out_rows[:, :, base + f0 : base + f1],
+                    in_=o[:].rearrange("p q c -> p (q c)")[:, f0:f1],
                 )
 
         def bias_rows():
@@ -290,21 +293,23 @@ def tile_hypconvhyperboloid_kernel(tc, x, W, b, out):
         transposes(2)
         stage(0, "v")
         stage(1, "a")
-        stage(2, "v")
-        for n in (0, 2, 4, 6):
+        for n in (0, 1, 2, 3):
             weight_tap(n)
         for n in CALLS:
             quant(0, n)
         weight_quant(0, 4)
-        for n in (1, 3, 5, 7):
-            weight_tap(n)
+        stage(2, "v")
+        weight_tap(4)
+        squares(1)
+        weight_tap(5)
+        sums(1)
+        roots(1)
+        weight_tap(6)
+        weight_tap(7)
         weight_quant(4, 8)
         weight_tap(8)
         weight_quant(8, 9)
         bias_rows()
-        squares(1)
-        sums(1)
-        roots(1)
 
         groups = len(GROUPS)
         staged = 3
@@ -318,25 +323,32 @@ def tile_hypconvhyperboloid_kernel(tc, x, W, b, out):
             bt = gi + 2
             for pp in new:
                 transposes(pp)
-            for m, pp in enumerate(new):
+            if bt < NCHUNK:
+                squares(bt)
+            if new:
+                stage(new[0], "a")
+            passes(gi, q0)
+            if bt < NCHUNK:
+                sums(bt)
+                roots(bt)
+            for pp in new[1:]:
                 stage(pp, "a")
-                if m == 0 and bt < NCHUNK:
-                    squares(bt)
             calls = CALLS if gi + 1 < groups else ()
             parts = width // 2
             for m in range(parts):
                 for n in calls[m * len(calls) // parts : (m + 1) * len(calls) // parts]:
                     quant(gi + 1, n)
                 if pending:
-                    finish_add(pending[0])
-                    finish_squares(pending[0])
+                    finish_add(pending[0][0], pending[0][1])
+                    finish_squares(pending[0][0], pending[0][1])
                     pending.remove(pending[0])
-                passes(gi, q0 + 2 * m)
-                passes(gi, q0 + 2 * m + 1)
-                pending.append(q0 // 2 + m)
-                if m == 0 and bt < NCHUNK:
-                    sums(bt)
-                    roots(bt)
-        for pp in pending:
-            finish_add(pp)
-            finish_squares(pp)
+                q = q0 + 2 * m
+                if m > 0:
+                    passes(gi, q)
+                if q >= ALONE:
+                    pending.append((q, 1))
+                passes(gi, q + 1)
+                pending.append((q + 1, 1) if q >= ALONE else (q, 2))
+        for q, n in pending:
+            finish_add(q, n)
+            finish_squares(q, n)

@@ -40,6 +40,7 @@ def tile_hypconvhyperboloid_kernel(tc, x, W, b, out):
         const = ctx.enter_context(tc.tile_pool(name="const", bufs=1))
         codes = ctx.enter_context(tc.tile_pool(name="codes", bufs=RING))
         outs = ctx.enter_context(tc.tile_pool(name="outs", bufs=2))
+        sorted_x = ctx.enter_context(tc.tile_pool(name="sorted_x", bufs=4))
         ps_tr = ctx.enter_context(tc.psum_pool(name="ps_tr", bufs=3))
         ps_misc = ctx.enter_context(tc.psum_pool(name="ps_misc", bufs=1))
         ps_z = ctx.enter_context(tc.psum_pool(name="ps_z", bufs=4))
@@ -159,13 +160,28 @@ def tile_hypconvhyperboloid_kernel(tc, x, W, b, out):
                         scale=1.0,
                     )
 
+        def sort_words(pp):
+            xd = sorted_x.tile([P, 2 * CPAD], BF16, tag="xd", name="xd")
+            state["xd%d" % pp] = xd
+            for k in range(2):
+                col = min(max(2 * pp - 1 + k, 0), NQ - 1)
+                c = max(i for i in range(NCHUNK) if CHUNKS[i] <= col)
+                xf = xs[c][:].bitcast(F32).rearrange("p (k w u) -> p k u w", w=P, u=2)
+                nc.scalar.copy(
+                    out=xd[:, k * CPAD : (k + 1) * CPAD].bitcast(F32).rearrange("p (u w) -> p u w", u=2),
+                    in_=xf[:, col - CHUNKS[c], :, :],
+                )
+
         def transposes(pp):
             tr = ps_tr.tile([P, 512], F32, tag="tr", name="tr")
             for k in range(2):
                 col = min(max(2 * pp - 1 + k, 0), NQ - 1)
                 for u in range(2):
                     s = 2 * k + u
-                    nc.tensor.transpose(tr[:, s * P : (s + 1) * P], x_words(col, u), permf[:])
+                    words = x_words(col, u)
+                    if ("xd%d" % pp) in state:
+                        words = state["xd%d" % pp][:].bitcast(F32)[:, s * P : (s + 1) * P]
+                    nc.tensor.transpose(tr[:, s * P : (s + 1) * P], words, permf[:])
             state["tr%d" % pp] = tr
 
         def copy_on(eng, dst, src):
@@ -314,12 +330,14 @@ def tile_hypconvhyperboloid_kernel(tc, x, W, b, out):
         groups = len(GROUPS)
         staged = 3
         pending = []
+        news = []
+        for gi in range(groups):
+            news.append(list(range(staged, last_pair(gi + 2) + 1)) if gi + 2 < groups else [])
+            staged += len(news[gi])
+        news.append([])
         for gi in range(groups):
             q0, width = GROUPS[gi]
-            new = []
-            if gi + 2 < groups:
-                new = list(range(staged, last_pair(gi + 2) + 1))
-                staged = last_pair(gi + 2) + 1
+            new = news[gi]
             bt = gi + 2
             for pp in new:
                 transposes(pp)
@@ -333,6 +351,9 @@ def tile_hypconvhyperboloid_kernel(tc, x, W, b, out):
                 roots(bt)
             for pp in new[1:]:
                 stage(pp, "a")
+            if gi + 1 >= 4:
+                for pp in news[gi + 1]:
+                    sort_words(pp)
             calls = CALLS if gi + 1 < groups else ()
             parts = width // 2
             for m in range(parts):

@@ -28,6 +28,7 @@ ORDER = (LENT,) + CALLS
 RING = 22
 WOFF = 16 * WIN
 ALONE = NQ - 2
+TSLOT = 480
 CUT = (ALONE % 8) * (OUT + 1) // 8 * 8
 
 FLOPS = 2 * 4096 * 4096 * 256
@@ -109,13 +110,7 @@ def tile_hypconvhyperboloid_kernel(tc, x, W, b, out):
         ones = const.tile([P, P], BF16, name="ones")
         nc.vector.memset(ones[:], 1.0)
 
-        wfirst = const.tile([P, 2], BF16, name="wfirst")
-        nc.gpsimd.tensor_copy(out=wfirst[:], in_=wv[:, 0, :, 0])
-        for n in range(TAPS):
-            if n == 4:
-                nc.gpsimd.tensor_copy(out=wv[:, n, :, 0], in_=wfirst[:])
-            else:
-                nc.gpsimd.memset(wv[:, n, :, 0], 0.0)
+        nc.gpsimd.tensor_copy(out=wv[:, 4, :, TSLOT], in_=wv[:, 0, :, 0])
 
         bbc = const.tile([P, 2 * OUT], F32, name="bbc")
         sq = const.tile([P, NQ + 2], F32, name="sq")
@@ -133,6 +128,7 @@ def tile_hypconvhyperboloid_kernel(tc, x, W, b, out):
 
         def squares(c):
             nc.scalar.activation(out=sq[:, 1 + CHUNKS[c] : 1 + CHUNKS[c + 1]], in_=xvs[c][:, :, 0], func=ACT.Square)
+            nc.scalar.activation(out=xvs[c][:, :, 0], in_=xvs[c][:, :, 0], func=ACT.Copy, scale=0.0)
             if c == 0:
                 nc.scalar.copy(out=sq[:, 0:1], in_=sq[:, 1:2])
             if c == NCHUNK - 1:
@@ -153,7 +149,7 @@ def tile_hypconvhyperboloid_kernel(tc, x, W, b, out):
                 a, e = max(lo, CHUNKS[c]), min(hi, CHUNKS[c + 1])
                 if a < e:
                     nc.scalar.activation(
-                        out=xvs[c][:, a - CHUNKS[c] : e - CHUNKS[c], 0],
+                        out=xvs[c][:, a - CHUNKS[c] : e - CHUNKS[c], TSLOT],
                         in_=state["sps%d" % bt][:, a - lo : e - lo],
                         func=ACT.Sqrt,
                         bias=neg8[:],

@@ -159,7 +159,7 @@ def tile_hypconvhyperboloid_kernel(tc, x, W, b, out):
         def sort_words(pp):
             xd = sorted_x.tile([P, 2 * CPAD], BF16, tag="xd", name="xd")
             state["xd%d" % pp] = xd
-            for k in range(2):
+            for k in range(1 if pp in (0, NCOL // 2 - 1) else 2):
                 col = min(max(2 * pp - 1 + k, 0), NQ - 1)
                 c = max(i for i in range(NCHUNK) if CHUNKS[i] <= col)
                 xf = xs[c][:].bitcast(F32).rearrange("p (k w u) -> p k u w", w=P, u=2)
@@ -170,7 +170,7 @@ def tile_hypconvhyperboloid_kernel(tc, x, W, b, out):
 
         def transposes(pp):
             tr = ps_tr.tile([P, 512], F32, tag="tr", name="tr")
-            for k in range(2):
+            for k in range(1 if pp in (0, NCOL // 2 - 1) else 2):
                 col = min(max(2 * pp - 1 + k, 0), NQ - 1)
                 for u in range(2):
                     s = 2 * k + u
@@ -187,12 +187,13 @@ def tile_hypconvhyperboloid_kernel(tc, x, W, b, out):
                 nc.scalar.copy(out=dst, in_=src)
 
         def stage(pp, eng):
-            tr = state["tr%d" % pp]
-            src = tr[:].rearrange("p (k u w) -> p k w u", k=2, u=2)
-            src6 = tr[:].rearrange("p (k u l b h) -> p k u l b h", k=2, u=2, l=16, b=4)
-            d32 = [wins[i][:, 2 * pp * WIN : (2 * pp + 2) * WIN].bitcast(F32) for i in range(3)]
-            dst = [d32[i].rearrange("p (k w u) -> p k w u", k=2, u=2) for i in range(3)]
-            dst6 = [d32[i].rearrange("p (k l b h u) -> p k l b h u", k=2, l=16, b=4, h=2) for i in range(3)]
+            c0, cols = (1, 1) if pp == 0 else (2 * pp, 1 if pp == NCOL // 2 - 1 else 2)
+            tr = state["tr%d" % pp][:, 0 : cols * 2 * P]
+            src = tr.rearrange("p (k u w) -> p k w u", k=cols, u=2)
+            src6 = tr.rearrange("p (k u l b h) -> p k u l b h", k=cols, u=2, l=16, b=4)
+            d32 = [wins[i][:, c0 * WIN : (c0 + cols) * WIN].bitcast(F32) for i in range(3)]
+            dst = [d32[i].rearrange("p (k w u) -> p k w u", k=cols, u=2) for i in range(3)]
+            dst6 = [d32[i].rearrange("p (k l b h u) -> p k l b h u", k=cols, l=16, b=4, h=2) for i in range(3)]
             copy_on(eng, dst[1], src)
             copy_on(eng, dst[0][:, :, 8:P, :], src[:, :, 0 : P - 8, :])
             copy_on(eng, dst6[0][:, :, 0, :, :, :], src6[:, :, :, 0:16:15, :, 0].rearrange("p k u l b -> p k b l u"))
@@ -223,14 +224,17 @@ def tile_hypconvhyperboloid_kernel(tc, x, W, b, out):
         def quant(gi, n):
             q0, width = GROUPS[gi]
             i, j = divmod(n, 3)
-            cod = codes.tile([P, width * P], U32, tag="cod", name="cod", align_bytes=64)
-            scl = codes.tile([P, width * P], U8, tag="scl", name="scl", align_bytes=64)
+            first, last = max(q0 + j, 1), min(q0 + j + width - 1, NQ)
+            cols = last - first + 1
+            cod = codes.tile([P, cols * P], U32, tag="cod", name="cod", align_bytes=64)
+            scl = codes.tile([P, cols * P], U8, tag="scl", name="scl", align_bytes=64)
             state[("cod", gi, n)] = cod
             state[("scl", gi, n)] = scl
+            state[("first", gi, n)] = first
             nc.vector.quantize_mx(
                 out=cod[:].bitcast(FP8X4),
                 scales=scl[:],
-                in_=wins[i][:, (q0 + j) * WIN : (q0 + j + width) * WIN],
+                in_=wins[i][:, first * WIN : (last + 1) * WIN],
             )
 
         def passes(gi, q):
@@ -241,11 +245,12 @@ def tile_hypconvhyperboloid_kernel(tc, x, W, b, out):
             z = state["z%d" % (q - half)]
             for n in ORDER:
                 s = n
-                src, w0 = (gi, n), (q - q0) * P
-                if n == LENT:
-                    left = max(q - 1, 0)
-                    gl = gi if left >= q0 else gi - 1
-                    src, w0 = (gl, LENT + 1), (left - GROUPS[gl][0]) * P
+                src, col = (gi, n), q + n % 3
+                if col < 1 or col > NQ:
+                    src, col = (gi, n - n % 3 + 1), q + 1
+                elif n == LENT:
+                    src = (gi if q > q0 else gi - 1, LENT + 1)
+                w0 = (col - state[("first",) + src]) * P
                 nc.tensor.matmul_mx(
                     out=z[:, half * OUT : (half + 1) * OUT],
                     lhsT=state[("cod",) + src][:, w0 : w0 + P].bitcast(FP8X4),
@@ -305,21 +310,23 @@ def tile_hypconvhyperboloid_kernel(tc, x, W, b, out):
         transposes(2)
         stage(0, "v")
         stage(1, "a")
-        for n in (0, 1, 2, 3):
-            weight_tap(n)
+        weight_tap(0, "v")
+        weight_tap(1, "a")
+        weight_tap(2, "a")
+        weight_tap(3, "a")
         for n in CALLS:
             quant(0, n)
         weight_quant(0, 4)
         stage(2, "v")
-        weight_tap(4)
+        weight_tap(4, "a")
         squares(1)
-        weight_tap(5)
+        weight_tap(5, "a")
         sums(1)
         roots(1)
-        weight_tap(6)
-        weight_tap(7)
+        weight_tap(6, "a")
+        weight_tap(7, "a")
         weight_quant(4, 8)
-        weight_tap(8)
+        weight_tap(8, "a")
         weight_quant(8, 9)
         bias_rows()
 

@@ -283,12 +283,15 @@ def tile_hypconvhyperboloid_kernel(tc, x, W, b, out):
                     out=junk[:], in_=o[:, k, 1 : OUT + 1], func=ACT.Square, accum_out=ss[:, k : k + 1]
                 )
             done = q + n
-            if done % 8 == 0 or done == ALONE:
-                k0, f0 = (ALONE % 8, CUT) if done == NQ else (0, 0)
-                k1, f1 = (ALONE % 8, CUT) if done == ALONE else (8, 8 * (OUT + 1))
+            if done % 8 == 0 or done >= ALONE:
+                k0 = 0 if done <= ALONE else (done - 1) % 8
+                k1 = (done - 1) % 8 + 1
+                f0 = k0 * (OUT + 1) // 8 * 8
+                f1 = k1 * (OUT + 1) // 8 * 8
                 base = (done - 1) // 8 * 8 * (OUT + 1)
                 nc.scalar.activation(out=o[:, k0:k1, 0], in_=ss[:, k0:k1], func=ACT.Sqrt, bias=one1[:], scale=1.0)
-                nc.sync.dma_start(
+                queue = nc.scalar if done == NQ else nc.sync
+                queue.dma_start(
                     out=out_rows[:, :, base + f0 : base + f1],
                     in_=o[:].rearrange("p q c -> p (q c)")[:, f0:f1],
                 )
@@ -354,7 +357,7 @@ def tile_hypconvhyperboloid_kernel(tc, x, W, b, out):
                 roots(bt)
             for pp in new[1:]:
                 stage(pp, "a")
-            if gi + 1 >= 4:
+            if gi + 1 >= 3:
                 for pp in news[gi + 1]:
                     sort_words(pp)
             calls = CALLS if gi + 1 < groups else ()

@@ -365,7 +365,7 @@ def tile_hypconvhyperboloid_kernel(tc, x, W, b, out):
             for m in range(parts):
                 for n in calls[m * len(calls) // parts : (m + 1) * len(calls) // parts]:
                     quant(gi + 1, n)
-                if pending:
+                if len(pending) > 1:
                     finish_add(pending[0][0], pending[0][1])
                     finish_squares(pending[0][0], pending[0][1])
                     pending.remove(pending[0])

@@ -25,6 +25,7 @@ GROUPS = ((0, 2), (2, 2), (4, 4), (8, 4), (12, 4), (16, 4), (20, 4), (24, 4), (2
 CALLS = (0, 6, 4, 1, 7, 5, 2, 8)
 LENT = 3
 ORDER = (LENT,) + CALLS
+SPARE = (0, 1)
 RING = 22
 WOFF = 16 * WIN
 ALONE = NQ - 2
@@ -71,7 +72,7 @@ def tile_hypconvhyperboloid_kernel(tc, x, W, b, out):
         nc.vector.memset(brow[:], 0.0)
         nc.scalar.dma_start(out=brow[0:1, :], in_=b.unsqueeze(0))
         load_x(0)
-        nc.vector.memset(wv[:, :, :, CH:CPAD], 0.0)
+        nc.vector.memset(wv[:, :, :, CH:CPAD].bitcast(F32), 0.0)
         nc.sync.dma_start(out=wv[:, 0, :, 0:CH], in_=w_taps[:, :, 455 * 0 : 455 * 0 + CH])
         nc.sync.dma_start(out=wv[:, 1, :, 0:CH], in_=w_taps[:, :, 455 * 1 : 455 * 1 + CH])
         nc.sync.dma_start(out=wv[:, 2, :, 0:CH], in_=w_taps[:, :, 455 * 2 : 455 * 2 + CH])
@@ -168,17 +169,19 @@ def tile_hypconvhyperboloid_kernel(tc, x, W, b, out):
                     in_=xf[:, col - CHUNKS[c], :, :],
                 )
 
-        def transposes(pp):
-            tr = ps_tr.tile([P, 512], F32, tag="tr", name="tr")
+        def transposes(pp, odd_and_even=(0, 1)):
+            if ("tr%d" % pp) not in state:
+                tr = ps_tr.tile([P, 512], F32, tag="tr", name="tr")
+                state["tr%d" % pp] = tr
+            tr = state["tr%d" % pp]
             for k in range(1 if pp in (0, NCOL // 2 - 1) else 2):
                 col = min(max(2 * pp - 1 + k, 0), NQ - 1)
-                for u in range(2):
+                for u in odd_and_even:
                     s = 2 * k + u
                     words = x_words(col, u)
                     if ("xd%d" % pp) in state:
                         words = state["xd%d" % pp][:].bitcast(F32)[:, s * P : (s + 1) * P]
                     nc.tensor.transpose(tr[:, s * P : (s + 1) * P], words, permf[:])
-            state["tr%d" % pp] = tr
 
         def copy_on(eng, dst, src):
             if eng == "v":
@@ -195,19 +198,23 @@ def tile_hypconvhyperboloid_kernel(tc, x, W, b, out):
             dst = [d32[i].rearrange("p (k w u) -> p k w u", k=cols, u=2) for i in range(3)]
             dst6 = [d32[i].rearrange("p (k l b h u) -> p k l b h u", k=cols, l=16, b=4, h=2) for i in range(3)]
             copy_on(eng, dst[1], src)
-            copy_on(eng, dst[0][:, :, 8:P, :], src[:, :, 0 : P - 8, :])
             copy_on(eng, dst6[0][:, :, 0, :, :, :], src6[:, :, :, 0:16:15, :, 0].rearrange("p k u l b -> p k b l u"))
-            copy_on(eng, dst[2][:, :, 0 : P - 8, :], src[:, :, 8:P, :])
             copy_on(eng, dst6[2][:, :, 15, :, :, :], src6[:, :, :, 0:16:15, :, 1].rearrange("p k u l b -> p k b l u"))
+            copy_on(eng, dst[0][:, :, 8:P, :], src[:, :, 0 : P - 8, :])
+            copy_on(eng, dst[2][:, :, 0 : P - 8, :], src[:, :, 8:P, :])
 
-        def weight_tap(n, eng="a"):
-            wg32 = wg.bitcast(F32)
+        def weight_turn(n):
             tr = ps_z.tile([P, 512], F32, tag="z", name="trw")
             wf = wraw.bitcast(F32).rearrange("p (n t w u) -> p n t w u", t=2, w=P, u=2)
             for ot in range(2):
                 for u in range(2):
                     s = 2 * ot + u
                     nc.tensor.transpose(tr[:, s * P : (s + 1) * P], wf[:, n, ot, :, u], ident[:])
+            state["trw%d" % n] = tr
+
+        def weight_copy(n, eng="a"):
+            wg32 = wg.bitcast(F32)
+            tr = state["trw%d" % n]
             copy_on(
                 eng,
                 wg32[:, n * 512 : (n + 1) * 512].rearrange("p (t o u) -> p t o u", t=2, u=2),
@@ -237,6 +244,9 @@ def tile_hypconvhyperboloid_kernel(tc, x, W, b, out):
                 in_=wins[i][:, first * WIN : (last + 1) * WIN],
             )
 
+        def calls_of(gi):
+            return tuple(n for n in CALLS if not (n in (0, 6) and gi in SPARE))
+
         def passes(gi, q):
             q0 = GROUPS[gi][0]
             half = q % 2 if q < ALONE else 0
@@ -248,8 +258,8 @@ def tile_hypconvhyperboloid_kernel(tc, x, W, b, out):
                 src, col = (gi, n), q + n % 3
                 if col < 1 or col > NQ:
                     src, col = (gi, n - n % 3 + 1), q + 1
-                elif n == LENT:
-                    src = (gi if q > q0 else gi - 1, LENT + 1)
+                elif n == LENT or (n in (0, 6) and gi in SPARE):
+                    src = (gi if q > q0 else gi - 1, n + 1)
                 w0 = (col - state[("first",) + src]) * P
                 nc.tensor.matmul_mx(
                     out=z[:, half * OUT : (half + 1) * OUT],
@@ -306,30 +316,41 @@ def tile_hypconvhyperboloid_kernel(tc, x, W, b, out):
             return (GROUPS[gi][0] + GROUPS[gi][1] + 1) // 2
 
         squares(0)
+        transposes(0, (1,))
+        transposes(1, (1,))
         sums(0)
         roots(0)
-        transposes(0)
-        transposes(1)
-        transposes(2)
+        weight_turn(0)
+        transposes(2, (1,))
+        transposes(0, (0,))
         stage(0, "v")
+        transposes(1, (0,))
         stage(1, "a")
-        weight_tap(0, "v")
-        weight_tap(1, "a")
-        weight_tap(2, "a")
-        weight_tap(3, "a")
-        for n in CALLS:
-            quant(0, n)
+        transposes(2, (0,))
+        weight_copy(0, "v")
+        weight_turn(1)
+        weight_copy(1)
+        weight_turn(2)
+        weight_copy(2)
+        weight_turn(3)
+        weight_copy(3)
+        for n in calls_of(0): quant(0, n)
         weight_quant(0, 4)
         stage(2, "v")
-        weight_tap(4, "a")
+        weight_turn(4)
+        weight_copy(4)
         squares(1)
-        weight_tap(5, "a")
+        weight_turn(5)
+        weight_copy(5)
         sums(1)
         roots(1)
-        weight_tap(6, "a")
-        weight_tap(7, "a")
+        weight_turn(6)
+        weight_copy(6)
+        weight_turn(7)
+        weight_copy(7)
         weight_quant(4, 8)
-        weight_tap(8, "a")
+        weight_turn(8)
+        weight_copy(8)
         weight_quant(8, 9)
         bias_rows()
 
@@ -360,7 +381,7 @@ def tile_hypconvhyperboloid_kernel(tc, x, W, b, out):
             if gi + 1 >= 3:
                 for pp in news[gi + 1]:
                     sort_words(pp)
-            calls = CALLS if gi + 1 < groups else ()
+            calls = calls_of(gi + 1) if gi + 1 < groups else ()
             parts = width // 2
             for m in range(parts):
                 for n in calls[m * len(calls) // parts : (m + 1) * len(calls) // parts]:

@@ -27,6 +27,7 @@ LENT = 3
 ORDER = (LENT,) + CALLS
 SPARE = (0, 1)
 RING = 22
+WIDE = 5
 WOFF = 16 * WIN
 ALONE = NQ - 2
 TSLOT = 480
@@ -72,21 +73,12 @@ def tile_hypconvhyperboloid_kernel(tc, x, W, b, out):
         nc.vector.memset(brow[:], 0.0)
         nc.scalar.dma_start(out=brow[0:1, :], in_=b.unsqueeze(0))
         load_x(0)
-        nc.vector.memset(wv[:, :, :, CH:CPAD].bitcast(F32), 0.0)
-        nc.sync.dma_start(out=wv[:, 0, :, 0:CH], in_=w_taps[:, :, 455 * 0 : 455 * 0 + CH])
-        nc.sync.dma_start(out=wv[:, 1, :, 0:CH], in_=w_taps[:, :, 455 * 1 : 455 * 1 + CH])
-        nc.sync.dma_start(out=wv[:, 2, :, 0:CH], in_=w_taps[:, :, 455 * 2 : 455 * 2 + CH])
-        nc.sync.dma_start(out=wv[:, 3, :, 0:CH], in_=w_taps[:, :, 455 * 3 : 455 * 3 + CH])
-        nc.sync.dma_start(out=wv[:, 4, :, 0:CH], in_=w_taps[:, :, 455 * 4 : 455 * 4 + CH])
-        load_x(1)
-        nc.sync.dma_start(out=wv[:, 5, :, 0:CH], in_=w_taps[:, :, 455 * 5 : 455 * 5 + CH])
-        nc.sync.dma_start(out=wv[:, 6, :, 0:CH], in_=w_taps[:, :, 455 * 6 : 455 * 6 + CH])
-        nc.sync.dma_start(out=wv[:, 7, :, 0:CH], in_=w_taps[:, :, 455 * 7 : 455 * 7 + CH])
-        nc.sync.dma_start(out=wv[:, 8, :, 0:CH], in_=w_taps[:, :, 455 * 8 : 455 * 8 + CH])
-        load_x(2)
-        load_x(3)
-        load_x(4)
-
+        nc.vector.memset(wv[:, WIDE:TAPS, :, CH:CPAD].bitcast(F32), 0.0)
+        nc.sync.dma_start(out=wv[:, 0, :, :], in_=w_taps[:, :, 455 * 0 : 455 * 0 + CPAD])
+        nc.sync.dma_start(out=wv[:, 1, :, :], in_=w_taps[:, :, 455 * 1 : 455 * 1 + CPAD])
+        nc.sync.dma_start(out=wv[:, 2, :, :], in_=w_taps[:, :, 455 * 2 : 455 * 2 + CPAD])
+        nc.sync.dma_start(out=wv[:, 3, :, :], in_=w_taps[:, :, 455 * 3 : 455 * 3 + CPAD])
+        nc.sync.dma_start(out=wv[:, 4, :, :], in_=w_taps[:, :, 455 * 4 : 455 * 4 + CPAD])
         one1 = const.tile([P, 1], F32, name="one1")
         nc.vector.memset(one1[:], 1.0)
         neg8 = const.tile([P, 1], F32, name="neg8")
@@ -111,10 +103,24 @@ def tile_hypconvhyperboloid_kernel(tc, x, W, b, out):
         ones = const.tile([P, P], BF16, name="ones")
         nc.vector.memset(ones[:], 1.0)
 
-        nc.gpsimd.tensor_copy(out=wv[:, 4, :, TSLOT], in_=wv[:, 0, :, 0])
+        load_x(1)
+        nc.sync.dma_start(out=wv[:, 5, :, 0:CH], in_=w_taps[:, :, 455 * 5 : 455 * 5 + CH])
+        nc.sync.dma_start(out=wv[:, 6, :, 0:CH], in_=w_taps[:, :, 455 * 6 : 455 * 6 + CH])
+        nc.sync.dma_start(out=wv[:, 7, :, 0:CH], in_=w_taps[:, :, 455 * 7 : 455 * 7 + CH])
+        nc.sync.dma_start(out=wv[:, 8, :, 0:CH], in_=w_taps[:, :, 455 * 8 : 455 * 8 + CH])
+        load_x(2)
+        load_x(3)
+        load_x(4)
+
+        for n in range(WIDE):
+            if n == 4:
+                nc.gpsimd.tensor_copy(out=wv[:, 4, :, TSLOT], in_=wv[:, 0, :, 0])
+            else:
+                nc.gpsimd.memset(wv[:, n, :, TSLOT], 0.0)
 
         bbc = const.tile([P, 2 * OUT], F32, name="bbc")
         sq = const.tile([P, NQ + 2], F32, name="sq")
+        sums3 = const.tile([P, CHUNKS[1]], F32, name="sums3")
         wc = const.tile([P, TAPS * OUT], U32, name="wc", align_bytes=64)
         ws = const.tile([P, TAPS * OUT], U8, name="ws", align_bytes=64)
         state = {}
@@ -129,18 +135,25 @@ def tile_hypconvhyperboloid_kernel(tc, x, W, b, out):
 
         def squares(c):
             nc.scalar.activation(out=sq[:, 1 + CHUNKS[c] : 1 + CHUNKS[c + 1]], in_=xvs[c][:, :, 0], func=ACT.Square)
-            nc.scalar.activation(out=xvs[c][:, :, 0], in_=xvs[c][:, :, 0], func=ACT.Copy, scale=0.0)
             if c == 0:
-                nc.scalar.copy(out=sq[:, 0:1], in_=sq[:, 1:2])
+                nc.scalar.activation(out=sq[:, 0:1], in_=xvs[c][:, 0:1, 0], func=ACT.Square)
             if c == NCHUNK - 1:
-                nc.scalar.copy(out=sq[:, NQ + 1 : NQ + 2], in_=sq[:, NQ : NQ + 1])
+                last = CHUNKS[NCHUNK] - CHUNKS[c] - 1
+                nc.scalar.activation(out=sq[:, NQ + 1 : NQ + 2], in_=xvs[c][:, last : last + 1, 0], func=ACT.Square)
+            nc.scalar.activation(out=xvs[c][:, :, 0], in_=xvs[c][:, :, 0], func=ACT.Copy, scale=0.0)
 
         def sums(bt):
             lo, hi = batch(bt)
             sps = ps_misc.tile([P, 512], F32, tag="misc", name="sps")
-            for j in range(3):
+            terms = [sq[:, lo + j : hi + j] for j in range(3)]
+            if bt == 0:
+                s3 = sums3[:, 0 : hi - lo]
+                nc.vector.tensor_tensor(out=s3, in0=terms[0], in1=terms[1], op=ALU.add)
+                nc.vector.tensor_tensor(out=s3, in0=s3, in1=terms[2], op=ALU.add)
+                terms = [s3]
+            for j, term in enumerate(terms):
                 nc.tensor.matmul(
-                    out=sps[:, 0 : hi - lo], lhsT=band[:], rhs=sq[:, lo + j : hi + j], start=(j == 0), stop=(j == 2)
+                    out=sps[:, 0 : hi - lo], lhsT=band[:], rhs=term, start=(j == 0), stop=(j == len(terms) - 1)
                 )
             state["sps%d" % bt] = sps
 
@@ -318,10 +331,10 @@ def tile_hypconvhyperboloid_kernel(tc, x, W, b, out):
         squares(0)
         transposes(0, (1,))
         transposes(1, (1,))
+        transposes(2, (1,))
         sums(0)
         roots(0)
         weight_turn(0)
-        transposes(2, (1,))
         transposes(0, (0,))
         stage(0, "v")
         transposes(1, (0,))
@@ -342,10 +355,10 @@ def tile_hypconvhyperboloid_kernel(tc, x, W, b, out):
         squares(1)
         weight_turn(5)
         weight_copy(5)
-        sums(1)
-        roots(1)
         weight_turn(6)
+        sums(1)
         weight_copy(6)
+        roots(1)
         weight_turn(7)
         weight_copy(7)
         weight_quant(4, 8)

from contextlib import ExitStack

import concourse.mybir as mybir
from concourse.masks import make_identity

F32 = mybir.dt.float32
BF16 = mybir.dt.bfloat16
U32 = mybir.dt.uint32
U8 = mybir.dt.uint8
FP8X4 = mybir.dt.float8_e4m3fn_x4
ACT = mybir.ActivationFunctionType
ALU = mybir.AluOpType

P = 128
NQ = 32
CH = 456
CPAD = 512
OUT = 256
TAPS = 9
WIN = 512
NCOL = NQ + 2
CHUNKS = (0, 6, 10, 18, 26, 32)
NCHUNK = 5
GROUPS = ((0, 2), (2, 2), (4, 4), (8, 4), (12, 4), (16, 4), (20, 4), (24, 4), (28, 2), (30, 2))
CALLS = (0, 6, 4, 1, 7, 5, 2, 8)
LENT = 3
ORDER = (LENT,) + CALLS
SPARE = (0, 1)
RING = 22
WIDE = 5
WOFF = 16 * WIN
ALONE = NQ - 2
TSLOT = 480
CUT = (ALONE % 8) * (OUT + 1) // 8 * 8

FLOPS = 2 * 4096 * 4096 * 256


def tile_hypconvhyperboloid_kernel(tc, x, W, b, out):
    nc = tc.nc
    with ExitStack() as ctx:
        ctx.enter_context(tc.manual_schedule())
        const = ctx.enter_context(tc.tile_pool(name="const", bufs=1))
        codes = ctx.enter_context(tc.tile_pool(name="codes", bufs=RING))
        outs = ctx.enter_context(tc.tile_pool(name="outs", bufs=2))
        sorted_x = ctx.enter_context(tc.tile_pool(name="sorted_x", bufs=4))
        ps_tr = ctx.enter_context(tc.psum_pool(name="ps_tr", bufs=3))
        ps_misc = ctx.enter_context(tc.psum_pool(name="ps_misc", bufs=1))
        ps_z = ctx.enter_context(tc.psum_pool(name="ps_z", bufs=4))

        x_rows = x.rearrange("b r q c -> (b r) q c")
        out_rows = out.rearrange("b (h l) q c -> l (b h) (q c)", h=2, l=16)

        xs = []
        for c in range(NCHUNK):
            xt = const.tile([P, (CHUNKS[c + 1] - CHUNKS[c]) * CPAD], BF16, name="x%d" % c)
            xs.append(xt)
        xvs = [xs[c][:].rearrange("p (k c) -> p k c", c=CPAD) for c in range(NCHUNK)]
        wins = []
        for i in range(3):
            wt = const.tile([P, NCOL * WIN], BF16, name="win%d" % i, align_bytes=64)
            wins.append(wt)
        wraw = wins[0][:, WOFF : WOFF + 2 * TAPS * CPAD]
        wv = wraw.rearrange("p (n t c) -> p n t c", t=2, c=CPAD)
        w_taps = W.rearrange("(t o) k -> o t k", t=2)
        wg = wins[1][:, WOFF : WOFF + TAPS * OUT * 4]

        def load_x(c):
            nc.vector.memset(xvs[c][:, :, CH:CPAD], 0.0)
            nc.sync.dma_start(out=xvs[c][:, :, 0:CH], in_=x_rows[:, CHUNKS[c] : CHUNKS[c + 1], :])

        brow = const.tile([P, OUT], BF16, name="brow")
        nc.vector.memset(brow[:], 0.0)
        nc.scalar.dma_start(out=brow[0:1, :], in_=b.unsqueeze(0))
        load_x(0)
        nc.vector.memset(wv[:, WIDE:TAPS, :, CH:CPAD].bitcast(F32), 0.0)
        nc.sync.dma_start(out=wv[:, 0, :, :], in_=w_taps[:, :, 455 * 0 : 455 * 0 + CPAD])
        nc.sync.dma_start(out=wv[:, 1, :, :], in_=w_taps[:, :, 455 * 1 : 455 * 1 + CPAD])
        nc.sync.dma_start(out=wv[:, 2, :, :], in_=w_taps[:, :, 455 * 2 : 455 * 2 + CPAD])
        nc.sync.dma_start(out=wv[:, 3, :, :], in_=w_taps[:, :, 455 * 3 : 455 * 3 + CPAD])
        nc.sync.dma_start(out=wv[:, 4, :, :], in_=w_taps[:, :, 455 * 4 : 455 * 4 + CPAD])
        one1 = const.tile([P, 1], F32, name="one1")
        nc.vector.memset(one1[:], 1.0)
        neg8 = const.tile([P, 1], F32, name="neg8")
        nc.vector.memset(neg8[:], -8.0)
        warm = const.tile([P, 1], F32, name="warm")
        nc.scalar.activation(out=warm[:], in_=one1[:], func=ACT.Sqrt)

        ident = const.tile([P, P], F32, name="ident")
        make_identity(nc, ident[:])
        permf = const.tile([P, P], F32, name="permf")
        nc.vector.tensor_copy(
            out=permf[:].rearrange("k (l g) -> k l g", g=8),
            in_=ident[:].rearrange("k (g l) -> k l g", l=16),
        )
        band = const.tile([P, P], F32, name="band")
        bv = band[:].rearrange("k (b r) -> k b r", r=32)
        iv = ident[:].rearrange("k (b r) -> k b r", r=32)
        nc.vector.tensor_copy(out=band[:], in_=ident[:])
        nc.vector.tensor_tensor(out=bv[:, :, 1:32], in0=bv[:, :, 1:32], in1=iv[:, :, 0:31], op=ALU.add)
        nc.vector.tensor_tensor(out=bv[:, :, 0:31], in0=bv[:, :, 0:31], in1=iv[:, :, 1:32], op=ALU.add)
        nc.vector.tensor_tensor(out=bv[:, :, 0:32:31], in0=bv[:, :, 0:32:31], in1=iv[:, :, 0:32:31], op=ALU.add)
        ones = const.tile([P, P], BF16, name="ones")
        nc.vector.memset(ones[:], 1.0)

        load_x(1)
        nc.sync.dma_start(out=wv[:, 5, :, 0:CH], in_=w_taps[:, :, 455 * 5 : 455 * 5 + CH])
        nc.sync.dma_start(out=wv[:, 6, :, 0:CH], in_=w_taps[:, :, 455 * 6 : 455 * 6 + CH])
        nc.sync.dma_start(out=wv[:, 7, :, 0:CH], in_=w_taps[:, :, 455 * 7 : 455 * 7 + CH])
        nc.sync.dma_start(out=wv[:, 8, :, 0:CH], in_=w_taps[:, :, 455 * 8 : 455 * 8 + CH])
        load_x(2)
        load_x(3)
        load_x(4)

        for n in range(WIDE):
            if n == 4:
                nc.gpsimd.tensor_copy(out=wv[:, 4, :, TSLOT], in_=wv[:, 0, :, 0])
            else:
                nc.gpsimd.memset(wv[:, n, :, TSLOT], 0.0)

        bbc = const.tile([P, 2 * OUT], F32, name="bbc")
        sq = const.tile([P, NQ + 2], F32, name="sq")
        sums3 = const.tile([P, CHUNKS[1]], F32, name="sums3")
        wc = const.tile([P, TAPS * OUT], U32, name="wc", align_bytes=64)
        ws = const.tile([P, TAPS * OUT], U8, name="ws", align_bytes=64)
        state = {}

        def batch(bt):
            return max(CHUNKS[bt] - 1, 0), (CHUNKS[bt + 1] - 1 if bt < NCHUNK - 1 else NQ)

        def x_words(col, u):
            c = max(i for i in range(NCHUNK) if CHUNKS[i] <= col)
            xf = xs[c][:].bitcast(F32).rearrange("p (k w u) -> p k w u", w=P, u=2)
            return xf[:, col - CHUNKS[c], :, u]

        def squares(c):
            nc.scalar.activation(out=sq[:, 1 + CHUNKS[c] : 1 + CHUNKS[c + 1]], in_=xvs[c][:, :, 0], func=ACT.Square)
            if c == 0:
                nc.scalar.activation(out=sq[:, 0:1], in_=xvs[c][:, 0:1, 0], func=ACT.Square)
            if c == NCHUNK - 1:
                last = CHUNKS[NCHUNK] - CHUNKS[c] - 1
                nc.scalar.activation(out=sq[:, NQ + 1 : NQ + 2], in_=xvs[c][:, last : last + 1, 0], func=ACT.Square)
            nc.scalar.activation(out=xvs[c][:, :, 0], in_=xvs[c][:, :, 0], func=ACT.Copy, scale=0.0)

        def sums(bt):
            lo, hi = batch(bt)
            sps = ps_misc.tile([P, 512], F32, tag="misc", name="sps")
            terms = [sq[:, lo + j : hi + j] for j in range(3)]
            if bt == 0:
                s3 = sums3[:, 0 : hi - lo]
                nc.vector.tensor_tensor(out=s3, in0=terms[0], in1=terms[1], op=ALU.add)
                nc.vector.tensor_tensor(out=s3, in0=s3, in1=terms[2], op=ALU.add)
                terms = [s3]
            for j, term in enumerate(terms):
                nc.tensor.matmul(
                    out=sps[:, 0 : hi - lo], lhsT=band[:], rhs=term, start=(j == 0), stop=(j == len(terms) - 1)
                )
            state["sps%d" % bt] = sps

        def roots(bt):
            lo, hi = batch(bt)
            for c in range(NCHUNK):
                a, e = max(lo, CHUNKS[c]), min(hi, CHUNKS[c + 1])
                if a < e:
                    nc.scalar.activation(
                        out=xvs[c][:, a - CHUNKS[c] : e - CHUNKS[c], TSLOT],
                        in_=state["sps%d" % bt][:, a - lo : e - lo],
                        func=ACT.Sqrt,
                        bias=neg8[:],
                        scale=1.0,
                    )

        def sort_words(pp):
            xd = sorted_x.tile([P, 2 * CPAD], BF16, tag="xd", name="xd")
            state["xd%d" % pp] = xd
            for k in range(1 if pp in (0, NCOL // 2 - 1) else 2):
                col = min(max(2 * pp - 1 + k, 0), NQ - 1)
                c = max(i for i in range(NCHUNK) if CHUNKS[i] <= col)
                xf = xs[c][:].bitcast(F32).rearrange("p (k w u) -> p k u w", w=P, u=2)
                nc.scalar.copy(
                    out=xd[:, k * CPAD : (k + 1) * CPAD].bitcast(F32).rearrange("p (u w) -> p u w", u=2),
                    in_=xf[:, col - CHUNKS[c], :, :],
                )

        def transposes(pp, odd_and_even=(0, 1)):
            if ("tr%d" % pp) not in state:
                tr = ps_tr.tile([P, 512], F32, tag="tr", name="tr")
                state["tr%d" % pp] = tr
            tr = state["tr%d" % pp]
            for k in range(1 if pp in (0, NCOL // 2 - 1) else 2):
                col = min(max(2 * pp - 1 + k, 0), NQ - 1)
                for u in odd_and_even:
                    s = 2 * k + u
                    words = x_words(col, u)
                    if ("xd%d" % pp) in state:
                        words = state["xd%d" % pp][:].bitcast(F32)[:, s * P : (s + 1) * P]
                    nc.tensor.transpose(tr[:, s * P : (s + 1) * P], words, permf[:])

        def copy_on(eng, dst, src):
            if eng == "v":
                nc.vector.tensor_copy(out=dst, in_=src)
            else:
                nc.scalar.copy(out=dst, in_=src)

        def stage(pp, eng):
            c0, cols = (1, 1) if pp == 0 else (2 * pp, 1 if pp == NCOL // 2 - 1 else 2)
            tr = state["tr%d" % pp][:, 0 : cols * 2 * P]
            src = tr.rearrange("p (k u w) -> p k w u", k=cols, u=2)
            src6 = tr.rearrange("p (k u l b h) -> p k u l b h", k=cols, u=2, l=16, b=4)
            d32 = [wins[i][:, c0 * WIN : (c0 + cols) * WIN].bitcast(F32) for i in range(3)]
            dst = [d32[i].rearrange("p (k w u) -> p k w u", k=cols, u=2) for i in range(3)]
            dst6 = [d32[i].rearrange("p (k l b h u) -> p k l b h u", k=cols, l=16, b=4, h=2) for i in range(3)]
            copy_on(eng, dst[1], src)
            copy_on(eng, dst6[0][:, :, 0, :, :, :], src6[:, :, :, 0:16:15, :, 0].rearrange("p k u l b -> p k b l u"))
            copy_on(eng, dst6[2][:, :, 15, :, :, :], src6[:, :, :, 0:16:15, :, 1].rearrange("p k u l b -> p k b l u"))
            copy_on(eng, dst[0][:, :, 8:P, :], src[:, :, 0 : P - 8, :])
            copy_on(eng, dst[2][:, :, 0 : P - 8, :], src[:, :, 8:P, :])

        def weight_turn(n):
            tr = ps_z.tile([P, 512], F32, tag="z", name="trw")
            wf = wraw.bitcast(F32).rearrange("p (n t w u) -> p n t w u", t=2, w=P, u=2)
            for ot in range(2):
                for u in range(2):
                    s = 2 * ot + u
                    nc.tensor.transpose(tr[:, s * P : (s + 1) * P], wf[:, n, ot, :, u], ident[:])
            state["trw%d" % n] = tr

        def weight_copy(n, eng="a"):
            wg32 = wg.bitcast(F32)
            tr = state["trw%d" % n]
            copy_on(
                eng,
                wg32[:, n * 512 : (n + 1) * 512].rearrange("p (t o u) -> p t o u", t=2, u=2),
                tr[:].rearrange("p (t u o) -> p t o u", t=2, u=2),
            )

        def weight_quant(s0, s1):
            nc.vector.quantize_mx(
                out=wc[:, s0 * OUT : s1 * OUT].bitcast(FP8X4),
                scales=ws[:, s0 * OUT : s1 * OUT],
                in_=wg[:, s0 * OUT * 4 : s1 * OUT * 4],
            )

        def quant(gi, n):
            q0, width = GROUPS[gi]
            i, j = divmod(n, 3)
            first, last = max(q0 + j, 1), min(q0 + j + width - 1, NQ)
            cols = last - first + 1
            cod = codes.tile([P, cols * P], U32, tag="cod", name="cod", align_bytes=64)
            scl = codes.tile([P, cols * P], U8, tag="scl", name="scl", align_bytes=64)
            state[("cod", gi, n)] = cod
            state[("scl", gi, n)] = scl
            state[("first", gi, n)] = first
            nc.vector.quantize_mx(
                out=cod[:].bitcast(FP8X4),
                scales=scl[:],
                in_=wins[i][:, first * WIN : (last + 1) * WIN],
            )

        def calls_of(gi):
            return tuple(n for n in CALLS if not (n in (0, 6) and gi in SPARE))

        def passes(gi, q):
            q0 = GROUPS[gi][0]
            half = q % 2 if q < ALONE else 0
            if half == 0:
                state["z%d" % q] = ps_z.tile([P, 512], F32, tag="z", name="z")
            z = state["z%d" % (q - half)]
            for n in ORDER:
                s = n
                src, col = (gi, n), q + n % 3
                if col < 1 or col > NQ:
                    src, col = (gi, n - n % 3 + 1), q + 1
                elif n == LENT or (n in (0, 6) and gi in SPARE):
                    src = (gi if q > q0 else gi - 1, n + 1)
                w0 = (col - state[("first",) + src]) * P
                nc.tensor.matmul_mx(
                    out=z[:, half * OUT : (half + 1) * OUT],
                    lhsT=state[("cod",) + src][:, w0 : w0 + P].bitcast(FP8X4),
                    lhsT_scale=state[("scl",) + src][:, w0 : w0 + P],
                    rhs=wc[:, s * OUT : (s + 1) * OUT].bitcast(FP8X4),
                    rhs_scale=ws[:, s * OUT : (s + 1) * OUT],
                    start=(n == ORDER[0]),
                    stop=(n == ORDER[TAPS - 1]),
                )

        def finish_add(q, n):
            s = q % 8
            if s == 0:
                state["o"] = outs.tile([P, 8, OUT + 1], F32, tag="o", name="o")
                state["ss"] = outs.tile([P, 8], F32, tag="ss", name="ss")
            nc.vector.tensor_tensor(
                out=state["o"][:, s : s + n, 1 : OUT + 1],
                in0=state["z%d" % q][:, 0 : n * OUT].rearrange("p (k n) -> p k n", k=n),
                in1=bbc[:, 0 : n * OUT].rearrange("p (k n) -> p k n", k=n),
                op=ALU.add,
            )

        def finish_squares(q, n):
            s = q % 8
            o = state["o"]
            ss = state["ss"]
            for k in range(s, s + n):
                junk = outs.tile([P, OUT], BF16, tag="junk", name="junk")
                nc.scalar.activation(
                    out=junk[:], in_=o[:, k, 1 : OUT + 1], func=ACT.Square, accum_out=ss[:, k : k + 1]
                )
            done = q + n
            if done % 8 == 0 or done >= ALONE:
                k0 = 0 if done <= ALONE else (done - 1) % 8
                k1 = (done - 1) % 8 + 1
                f0 = k0 * (OUT + 1) // 8 * 8
                f1 = k1 * (OUT + 1) // 8 * 8
                base = (done - 1) // 8 * 8 * (OUT + 1)
                nc.scalar.activation(out=o[:, k0:k1, 0], in_=ss[:, k0:k1], func=ACT.Sqrt, bias=one1[:], scale=1.0)
                queue = nc.scalar if done == NQ else nc.sync
                queue.dma_start(
                    out=out_rows[:, :, base + f0 : base + f1],
                    in_=o[:].rearrange("p q c -> p (q c)")[:, f0:f1],
                )

        def bias_rows():
            bps = ps_misc.tile([P, 512], F32, tag="misc", name="bps")
            nc.tensor.matmul(out=bps[:, 0:OUT], lhsT=ones[:], rhs=brow[:], start=True, stop=True)
            nc.scalar.copy(out=bbc[:, 0:OUT], in_=bps[:, 0:OUT])
            nc.scalar.copy(out=bbc[:, OUT : 2 * OUT], in_=bps[:, 0:OUT])

        def last_pair(gi):
            return (GROUPS[gi][0] + GROUPS[gi][1] + 1) // 2

        squares(0)
        transposes(0, (1,))
        transposes(1, (1,))
        transposes(2, (1,))
        sums(0)
        roots(0)
        weight_turn(0)
        transposes(0, (0,))
        stage(0, "v")
        transposes(1, (0,))
        stage(1, "a")
        transposes(2, (0,))
        weight_copy(0, "v")
        weight_turn(1)
        weight_copy(1)
        weight_turn(2)
        weight_copy(2)
        weight_turn(3)
        weight_copy(3)
        for n in calls_of(0): quant(0, n)
        weight_quant(0, 4)
        stage(2, "v")
        weight_turn(4)
        weight_copy(4)
        squares(1)
        weight_turn(5)
        weight_copy(5)
        weight_turn(6)
        sums(1)
        weight_copy(6)
        roots(1)
        weight_turn(7)
        weight_copy(7)
        weight_quant(4, 8)
        weight_turn(8)
        weight_copy(8)
        weight_quant(8, 9)
        bias_rows()

        groups = len(GROUPS)
        staged = 3
        pending = []
        news = []
        for gi in range(groups):
            news.append(list(range(staged, last_pair(gi + 2) + 1)) if gi + 2 < groups else [])
            staged += len(news[gi])
        news.append([])
        for gi in range(groups):
            q0, width = GROUPS[gi]
            new = news[gi]
            bt = gi + 2
            for pp in new:
                transposes(pp)
            if bt < NCHUNK:
                squares(bt)
            if new:
                stage(new[0], "a")
            passes(gi, q0)
            if bt < NCHUNK:
                sums(bt)
                roots(bt)
            for pp in new[1:]:
                stage(pp, "a")
            if gi + 1 >= 3:
                for pp in news[gi + 1]:
                    sort_words(pp)
            calls = calls_of(gi + 1) if gi + 1 < groups else ()
            parts = width // 2
            for m in range(parts):
                for n in calls[m * len(calls) // parts : (m + 1) * len(calls) // parts]:
                    quant(gi + 1, n)
                if len(pending) > 1:
                    finish_add(pending[0][0], pending[0][1])
                    finish_squares(pending[0][0], pending[0][1])
                    pending.remove(pending[0])
                q = q0 + 2 * m
                if m > 0:
                    passes(gi, q)
                if q >= ALONE:
                    pending.append((q, 1))
                passes(gi, q + 1)
                pending.append((q + 1, 1) if q >= ALONE else (q, 2))
        for q, n in pending:
            finish_add(q, n)
            finish_squares(q, n)
